import numpy as np
import ml_dtypes


def mxq(x, axis, fmt="e4m3"):
    dtype, down = {"e4m3": (ml_dtypes.float8_e4m3fn, 7), "e5m2": (ml_dtypes.float8_e5m2, 14)}[fmt]
    v = np.moveaxis(np.asarray(x, np.float32).astype(ml_dtypes.bfloat16).astype(np.float64), axis, -1)
    blocks = v.reshape(v.shape[:-1] + (-1, 32))
    amax = np.abs(blocks).max(-1, keepdims=True)
    byte = np.maximum(np.where(amax > 0, np.frexp(amax)[1] - 1 + 127, 0) - down, 1)
    scale = np.exp2(byte - 127.0)
    codes = (blocks / scale).astype(np.float32).astype(dtype).astype(np.float64)
    return np.moveaxis((codes * scale).reshape(v.shape), -1, axis)


WIDE = False


def mx_kscale(k):
    if not WIDE:
        return np.ones(k)
    levels = np.array([10, -10, 5, -5, 0])
    a = np.random.permutation(np.resize(levels, k // 512 * 4)).reshape(k // 512, 4)
    idx = np.arange(k)
    return np.exp2(a[idx // 512, idx % 128 // 32])


BF16 = ml_dtypes.bfloat16


def bf(x):
    return np.asarray(x, np.float32).astype(BF16)


def f64(x):
    return np.asarray(x).astype(np.float64)


B, C, C4, H, W, R = 1, 2048, 512, 32, 64, 4
ND = 2 * R + 1
GAIN = 1.2
QS = GAIN * C4 ** 0.25
BS = 0.3 * QS


def setup_inputs():
    s, t = mx_kscale(C), mx_kscale(C4)
    return {"x": bf(np.random.standard_normal((B, C, H, W)) * s[None, :, None, None]),
            "y": bf(np.random.standard_normal((B, C, H, W)) * s[None, :, None, None]),
            "query_w": bf(np.random.standard_normal((C4, C)) * QS / np.sqrt(C) * t[:, None] / s[None, :]),
            "query_b": bf(np.random.standard_normal(C4) * BS * t),
            "key_w": bf(np.random.standard_normal((C4, C)) * QS / np.sqrt(C) / t[:, None] / s[None, :]),
            "key_b": bf(np.random.standard_normal(C4) * BS / t)}


def reference(x, y, query_w, query_b, key_w, key_b):
    yq = mxq(f64(y).reshape(B, C, H * W), 1, "e4m3")
    xq = mxq(f64(x).reshape(B, C, H * W), 1, "e4m3")
    q = (mxq(f64(query_w), 1, "e4m3") @ yq) + f64(query_b)[None, :, None]
    k = (mxq(f64(key_w), 1, "e4m3") @ xq) + f64(key_b)[None, :, None]
    qq = mxq(q, 1, "e4m3").reshape(B, C4, H, W).transpose(0, 2, 3, 1)
    kq = mxq(k, 1, "e4m3").reshape(B, C4, H, W).transpose(0, 2, 1, 3)
    corr = np.zeros((B, H, W, ND * ND))
    for di in range(ND):
        oi = di - R
        i0, i1 = max(0, -oi), min(H, H - oi)
        sc = qq[:, i0:i1] @ kq[:, i0 + oi:i1 + oi]
        for dj in range(ND):
            oj = dj - R
            w0, w1 = max(0, -oj), min(W, W - oj)
            corr[:, i0:i1, w0:w1, di * ND + dj] = np.diagonal(sc, offset=oj, axis1=2, axis2=3)
    corr = corr / C4
    e = np.exp(corr - corr.max(-1, keepdims=True))
    return e / e.sum(-1, keepdims=True)

@@ -1,0 +1,234 @@
+from contextlib import ExitStack
+
+import concourse.mybir as mybir
+from concourse.masks import make_identity
+
+F32 = mybir.dt.float32
+BF16 = mybir.dt.bfloat16
+U32 = mybir.dt.uint32
+U8 = mybir.dt.uint8
+I32 = mybir.dt.int32
+FP8X4 = mybir.dt.float8_e4m3fn_x4
+ACT = mybir.ActivationFunctionType
+ALU = mybir.AluOpType
+AX = mybir.AxisListType
+
+P = 128
+C = 2048
+C4 = 512
+H = 32
+W = 64
+NPIX = H * W
+ND = 9
+NDD = ND * ND
+PASSES = C // 512
+UNIT = 512
+KPAD = 4 * W
+SW = 640
+RUN = 64 * (ND - 1) + ND
+SLOT_BASE = (64, 64 + P * SW + 128)
+
+FLOPS = 2 * 2 * C4 * C * NPIX + 2 * NPIX * NDD * C4
+
+SCALAR_CHUNKS = (1, 4, 6)
+
+
+def tile_local_module_pa_kernel(tc, x, y, query_w, query_b, key_w, key_b, out):
+    nc = tc.nc
+    xf = x.rearrange("b c h w -> (b c) (h w)")
+    yf = y.rearrange("b c h w -> (b c) (h w)")
+    flat = out.rearrange("b h w d -> (b h w d)")
+    out2d = out.rearrange("b h w d -> (b h w) d")
+
+    with ExitStack() as ctx:
+        const = ctx.enter_context(tc.tile_pool(name="const", bufs=1))
+        wraw = ctx.enter_context(tc.tile_pool(name="wraw", bufs=1))
+        wgrp = ctx.enter_context(tc.tile_pool(name="wgrp", bufs=2))
+        rawp = ctx.enter_context(tc.tile_pool(name="rawp", bufs=10))
+        grpp = ctx.enter_context(tc.tile_pool(name="grpp", bufs=4))
+        ucp = ctx.enter_context(tc.tile_pool(name="ucp", bufs=3))
+        pbp = ctx.enter_context(tc.tile_pool(name="pbp", bufs=2))
+        stp = ctx.enter_context(tc.tile_pool(name="stp", bufs=2))
+        rbp = ctx.enter_context(tc.tile_pool(name="rbp", bufs=3))
+        smp = ctx.enter_context(tc.tile_pool(name="smp", bufs=4))
+        psa = ctx.enter_context(tc.psum_pool(name="psa", bufs=4))
+        pss = ctx.enter_context(tc.psum_pool(name="pss", bufs=2))
+
+        ident = const.tile([P, P], F32, name="ident")
+        make_identity(nc, ident[:])
+        zero = const.tile([P, P], F32, name="zero")
+        nc.vector.memset(zero[:], 0.0)
+        for a, n in ((0, 64), (SLOT_BASE[0] + P * SW, 128), (SLOT_BASE[1] + P * SW, 128)):
+            nc.sync.dma_start(out=flat[a : a + n].rearrange("(o c) -> o c", o=1), in_=zero[0:1, 0:n])
+
+        ui = const.tile([P, ND], I32, name="ui")
+        nc.gpsimd.iota(ui[0:64, :], pattern=[[1, ND]], base=-4, channel_multiplier=1)
+        nc.gpsimd.iota(ui[64:128, :], pattern=[[1, ND]], base=-4, channel_multiplier=1)
+        uf = const.tile([P, ND], F32, name="uf")
+        nc.vector.tensor_copy(out=uf[:], in_=ui[:])
+        ma = const.tile([P, ND], F32, name="ma")
+        nc.vector.tensor_scalar(out=ma[:], in0=uf[:], scalar1=0.0, scalar2=1.0 / C4, op0=ALU.is_ge, op1=ALU.mult)
+        mb = const.tile([P, ND], F32, name="mb")
+        nc.vector.tensor_scalar(out=mb[:], in0=uf[:], scalar1=float(W - 1), scalar2=None, op0=ALU.is_le)
+        m9 = const.tile([P, ND], F32, name="m9")
+        nc.vector.tensor_tensor(out=m9[:], in0=ma[:], in1=mb[:], op=ALU.mult)
+        mask = const.tile([P, ND, ND], F32, name="mask")
+        nc.vector.tensor_copy(out=mask[:], in_=m9[:].unsqueeze(1).to_broadcast([P, ND, ND]))
+
+        qc = const.tile([P, NPIX], U32, name="qc", align_bytes=64)
+        qs = const.tile([P, NPIX], U8, name="qs", align_bytes=64)
+        kc = const.tile([P, NPIX + 2 * KPAD], U32, name="kc", align_bytes=64)
+        ks = const.tile([P, NPIX + 2 * KPAD], U8, name="ks", align_bytes=64)
+        nc.vector.memset(kc[:, 0:KPAD].bitcast(I32), 0)
+        nc.vector.memset(kc[:, KPAD + NPIX :].bitcast(I32), 0)
+        nc.vector.memset(ks[:, 0:KPAD].bitcast(I32), 0)
+        nc.vector.memset(ks[:, KPAD + NPIX :].bitcast(I32), 0)
+        res = const.tile([P, NPIX // P, NDD], F32, name="res")
+
+        state = {"chunk": 0, "evac": 0}
+
+        def copy_on(scalar_engine, dst, src):
+            if scalar_engine:
+                nc.scalar.copy(out=dst, in_=src)
+            else:
+                nc.vector.tensor_copy(out=dst, in_=src)
+
+        def prep_w(w_ap, b_ap, nm, pieces):
+            wsb = wraw.tile([P, 4, C], BF16, name="wsb_" + nm)
+            wv = w_ap.rearrange("(p m) c -> p m c", m=4)
+            step = C // pieces
+            for i in range(pieces):
+                nc.sync.dma_start(out=wsb[:, :, i * step : (i + 1) * step], in_=wv[:, :, i * step : (i + 1) * step])
+            bb = const.tile([P, 4], BF16, name="bb_" + nm)
+            nc.sync.dma_start(out=bb[:], in_=b_ap.rearrange("(p m) -> p m", m=4))
+            bias = const.tile([P, 4], F32, name="bias_" + nm)
+            nc.vector.tensor_copy(out=bias[:], in_=bb[:])
+            wc = const.tile([P, PASSES, C4], U32, name="wc_" + nm, align_bytes=64)
+            ws = const.tile([P, PASSES, C4], U8, name="ws_" + nm, align_bytes=64)
+            w32 = wsb[:].bitcast(F32)
+            for g in range(PASSES):
+                wg = wgrp.tile([P, 4 * C4], BF16, name="wg", align_bytes=64)
+                wg32 = wg[:].bitcast(F32)
+                for mm in range(2):
+                    pt = psa.tile([P, 512], F32, name="acc")
+                    for mi in range(2):
+                        for u in range(2):
+                            nc.tensor.transpose(
+                                pt[:, (2 * mi + u) * P : (2 * mi + u + 1) * P],
+                                w32[:, 2 * mm + mi, 256 * g + u : 256 * g + 256 : 2],
+                                ident[:],
+                            )
+                    state["evac"] += 1
+                    copy_on(
+                        state["evac"] % 2 == 0,
+                        wg32[:, 512 * mm : 512 * mm + 512].rearrange("p (mi c u) -> p mi c u", mi=2, u=2),
+                        pt[:].rearrange("p (mi u c) -> p mi c u", mi=2, u=2),
+                    )
+                nc.vector.quantize_mx(out=wc[:, g, :].bitcast(FP8X4), scales=ws[:, g, :], in_=wg[:])
+            return wc, ws, bias
+
+        def regroup(scalar_engine, dst, src):
+            copy_on(
+                scalar_engine,
+                dst.rearrange("p (c i t) -> p c t i", i=4, t=4),
+                src.rearrange("p t (c i) -> p c t i", i=4),
+            )
+
+        def unit(src2d, s, wpack, codes, scales):
+            wc, ws, bias = wpack
+            uc = ucp.tile([P, PASSES, UNIT], U32, name="uc", align_bytes=64)
+            us = ucp.tile([P, PASSES, UNIT], U8, name="us", align_bytes=64)
+            for g in range(PASSES):
+                raw = rawp.tile([P, 4, UNIT], BF16, name="raw")
+                nc.sync.dma_start(
+                    out=raw[:],
+                    in_=src2d[512 * g : 512 * g + 512, s : s + UNIT].rearrange("(p t) w -> p t w", t=4),
+                )
+                grp = grpp.tile([P, 4 * UNIT], BF16, name="grp", align_bytes=64)
+                regroup(state["chunk"] % 8 in SCALAR_CHUNKS, grp[:], raw[:])
+                state["chunk"] += 1
+                nc.vector.quantize_mx(out=uc[:, g, :].bitcast(FP8X4), scales=us[:, g, :], in_=grp[:])
+            accs = []
+            for m in range(4):
+                acc = psa.tile([P, UNIT], F32, name="acc")
+                accs.append(acc)
+            for g in range(PASSES):
+                for m in range(4):
+                    nc.tensor.matmul_mx(
+                        out=accs[m][:],
+                        lhsT=wc[:, g, P * m : P * m + P].bitcast(FP8X4),
+                        lhsT_scale=ws[:, g, P * m : P * m + P],
+                        rhs=uc[:, g, :].bitcast(FP8X4),
+                        rhs_scale=us[:, g, :],
+                        start=(g == 0),
+                        stop=(g == PASSES - 1),
+                    )
+            pb = pbp.tile([P, 4, UNIT], BF16, name="pb")
+            for m in range(4):
+                nc.scalar.activation(out=pb[:, m, :], in_=accs[m][:], func=ACT.Identity, bias=bias[:, m : m + 1], scale=1.0)
+            g2 = pbp.tile([P, 4 * UNIT], BF16, name="g2", align_bytes=64)
+            regroup(False, g2[:], pb[:])
+            nc.vector.quantize_mx(out=codes.bitcast(FP8X4), scales=scales, in_=g2[:])
+
+        def corr_tile(t):
+            sm = pss.tile([P, 512], F32, name="sm")
+            sr = pss.tile([P, P], F32, name="sr")
+            for dst, c0, n in ((sm, 0, 512), (sr, 512, P)):
+                nc.tensor.matmul_mx(
+                    out=dst[:],
+                    lhsT=qc[:, P * t : P * t + P].bitcast(FP8X4),
+                    lhsT_scale=qs[:, P * t : P * t + P],
+                    rhs=kc[:, P * t + c0 : P * t + c0 + n].bitcast(FP8X4),
+                    rhs_scale=ks[:, P * t + c0 : P * t + c0 + n],
+                    start=True,
+                    stop=True,
+                )
+            st = stp.tile([P, SW], F32, name="st")
+            nc.scalar.copy(out=st[:, 0:512], in_=sm[:])
+            nc.vector.tensor_copy(out=st[:, 512:SW], in_=sr[:])
+            base = SLOT_BASE[t % 2]
+            nc.sync.dma_start(out=flat[base : base + P * SW].rearrange("(m c) -> m c", c=SW), in_=st[:])
+            rb = rbp.tile([P, ND * 64], F32, name="rb")
+            nc.sync.dma_start(
+                out=rb[:, 0:RUN],
+                in_=flat[base - 4 : base - 4 + P * (SW + 1)].rearrange("(m c) -> m c", c=SW + 1)[:, 0:RUN],
+            )
+            corr = smp.tile([P, ND, ND], F32, name="corr")
+            nc.vector.tensor_tensor(
+                out=corr[:], in0=rb[:].rearrange("p (a c) -> p a c", c=64)[:, :, 0:ND], in1=mask[:], op=ALU.mult
+            )
+            nmx = smp.tile([P, 1], F32, name="nmx")
+            nc.vector.tensor_reduce(out=nmx[:], in_=corr[:].rearrange("p a d -> p (a d)"), axis=AX.X, op=ALU.max, negate=True)
+            ex = smp.tile([P, NDD], F32, name="ex")
+            den = smp.tile([P, 1], F32, name="den")
+            nc.scalar.activation(
+                out=ex[:], in_=corr[:].rearrange("p a d -> p (a d)"), func=ACT.Exp, bias=nmx[:, 0:1], scale=1.0, accum_out=den[:, 0:1]
+            )
+            rden = smp.tile([P, 1], F32, name="rden")
+            nc.vector.reciprocal(out=rden[:], in_=den[:])
+            nc.scalar.activation(out=res[:, t, :], in_=ex[:], func=ACT.Copy, scale=rden[:, 0:1])
+
+        def k_unit(b):
+            unit(xf, UNIT * b, wk, kc[:, KPAD + UNIT * b : KPAD + UNIT * (b + 1)], ks[:, KPAD + UNIT * b : KPAD + UNIT * (b + 1)])
+
+        def q_unit(b):
+            unit(yf, UNIT * b, wq, qc[:, UNIT * b : UNIT * (b + 1)], qs[:, UNIT * b : UNIT * (b + 1)])
+            for t in range(4 * b, 4 * b + 4):
+                corr_tile(t)
+
+        wk = prep_w(key_w, key_b, "k", 4)
+        k_unit(0)
+        wq = prep_w(query_w, query_b, "q", 1)
+        k_unit(1)
+        q_unit(0)
+        k_unit(2)
+        q_unit(1)
+        k_unit(3)
+        q_unit(2)
+        q_unit(3)
+
+        for hf in range(2):
+            nc.sync.dma_start(
+                out=out2d[1024 * hf : 1024 * hf + 1024, :].rearrange("(t m) d -> m t d", m=P),
+                in_=res[:, 8 * hf : 8 * hf + 8, :],
+            )

@@ -23,212 +23,357 @@ ND = 9
 NDD = ND * ND
 PASSES = C // 512
 UNIT = 512
-KPAD = 4 * W
-SW = 640
-RUN = 64 * (ND - 1) + ND
-SLOT_BASE = (64, 64 + P * SW + 128)
+TR = 8
+TJ = 16
+KE = 24
+KP = 32
+KROWS = H + 8
+SWID = (TR + 8) * KE
+RUN = KE * (ND - 1) + ND
+RSTEP = TJ * SWID + KE
+SLOT = TR * RSTEP
+NSLOT = 3
 
 FLOPS = 2 * 2 * C4 * C * NPIX + 2 * NPIX * NDD * C4
 
-SCALAR_CHUNKS = (1, 4, 6)
+VSPLIT = 328
+LOOKAHEAD = 17
+UNITS = (("k", 0), ("k", 1), ("q", 0), ("k", 2), ("q", 1), ("k", 3), ("q", 2), ("q", 3))
 
 
 def tile_local_module_pa_kernel(tc, x, y, query_w, query_b, key_w, key_b, out):
     nc = tc.nc
-    xf = x.rearrange("b c h w -> (b c) (h w)")
-    yf = y.rearrange("b c h w -> (b c) (h w)")
+    src2d = {"k": x.rearrange("b c h w -> (b c) (h w)"), "q": y.rearrange("b c h w -> (b c) (h w)")}
+    wv = {"k": key_w.rearrange("(p m) c -> p m c", m=4), "q": query_w.rearrange("(p m) c -> p m c", m=4)}
+    bv = {"k": key_b.rearrange("(p m) -> p m", m=4), "q": query_b.rearrange("(p m) -> p m", m=4)}
     flat = out.rearrange("b h w d -> (b h w d)")
     out2d = out.rearrange("b h w d -> (b h w) d")
 
+    items = []
+    for g in range(PASSES):
+        items.append(("x", 0, g))
+        items.append(("w", "k", g))
+    for g in range(PASSES):
+        items.append(("x", 1, g))
+        items.append(("w", "q", g))
+    for u in range(2, len(UNITS)):
+        for g in range(PASSES):
+            items.append(("x", u, g))
+
     with ExitStack() as ctx:
         const = ctx.enter_context(tc.tile_pool(name="const", bufs=1))
-        wraw = ctx.enter_context(tc.tile_pool(name="wraw", bufs=1))
-        wgrp = ctx.enter_context(tc.tile_pool(name="wgrp", bufs=2))
-        rawp = ctx.enter_context(tc.tile_pool(name="rawp", bufs=10))
-        grpp = ctx.enter_context(tc.tile_pool(name="grpp", bufs=4))
+        rawp = ctx.enter_context(tc.tile_pool(name="rawp", bufs=LOOKAHEAD + 1))
+        grpp = ctx.enter_context(tc.tile_pool(name="grpp", bufs=3))
         ucp = ctx.enter_context(tc.tile_pool(name="ucp", bufs=3))
         pbp = ctx.enter_context(tc.tile_pool(name="pbp", bufs=2))
-        stp = ctx.enter_context(tc.tile_pool(name="stp", bufs=2))
-        rbp = ctx.enter_context(tc.tile_pool(name="rbp", bufs=3))
+        stp = ctx.enter_context(tc.tile_pool(name="stp", bufs=4))
+        rbp = ctx.enter_context(tc.tile_pool(name="rbp", bufs=4))
         smp = ctx.enter_context(tc.tile_pool(name="smp", bufs=4))
         psa = ctx.enter_context(tc.psum_pool(name="psa", bufs=4))
+        pst = ctx.enter_context(tc.psum_pool(name="pst", bufs=2))
         pss = ctx.enter_context(tc.psum_pool(name="pss", bufs=2))
+        ctx.enter_context(tc.manual_schedule())
+
+        raws = {}
+        tps = {}
+        sched = {}
+        ucs = {}
+        accs = {}
+        pbs = {}
+        g2s = {}
+        sms = {}
+        sts = {}
+        rbs = {}
+        soft = {}
+        wready = {}
+        for i in range(len(items)):
+            if items[i][0] == "w" and items[i][2] == PASSES - 1:
+                wready[items[i][1]] = i + 1
+        rslot = {}
+
+        def at(slot, fn):
+            if slot not in sched:
+                sched[slot] = []
+            sched[slot].append(fn)
+
+        def emit_load(i):
+            kind, a, g = items[i]
+            raw = rawp.tile([P, 4, UNIT], BF16, name="raw")
+            raws[i] = raw
+            if kind == "x":
+                nm, b = UNITS[a]
+                nc.sync.dma_start(
+                    out=raw[:],
+                    in_=src2d[nm][512 * g : 512 * g + 512, UNIT * b : UNIT * (b + 1)].rearrange("(p t) w -> p t w", t=4),
+                )
+            else:
+                nc.sync.dma_start(out=raw[:], in_=wv[a][:, :, 512 * g : 512 * g + 512])
 
         ident = const.tile([P, P], F32, name="ident")
         make_identity(nc, ident[:])
-        zero = const.tile([P, P], F32, name="zero")
-        nc.vector.memset(zero[:], 0.0)
-        for a, n in ((0, 64), (SLOT_BASE[0] + P * SW, 128), (SLOT_BASE[1] + P * SW, 128)):
-            nc.sync.dma_start(out=flat[a : a + n].rearrange("(o c) -> o c", o=1), in_=zero[0:1, 0:n])
+        bias = {}
+        bbs = {}
+        for nm in ("k", "q"):
+            bbs[nm] = const.tile([P, 4], BF16, name="bb_" + nm)
+            nc.scalar.dma_start(out=bbs[nm][:], in_=bv[nm])
+            bias[nm] = const.tile([P, 4], F32, name="bias_" + nm)
+            at(6, lambda nm=nm: nc.vector.tensor_copy(out=bias[nm][:], in_=bbs[nm][:]))
+        for i in range(LOOKAHEAD):
+            emit_load(i)
 
-        ui = const.tile([P, ND], I32, name="ui")
-        nc.gpsimd.iota(ui[0:64, :], pattern=[[1, ND]], base=-4, channel_multiplier=1)
-        nc.gpsimd.iota(ui[64:128, :], pattern=[[1, ND]], base=-4, channel_multiplier=1)
-        uf = const.tile([P, ND], F32, name="uf")
-        nc.vector.tensor_copy(out=uf[:], in_=ui[:])
-        ma = const.tile([P, ND], F32, name="ma")
-        nc.vector.tensor_scalar(out=ma[:], in0=uf[:], scalar1=0.0, scalar2=1.0 / C4, op0=ALU.is_ge, op1=ALU.mult)
-        mb = const.tile([P, ND], F32, name="mb")
-        nc.vector.tensor_scalar(out=mb[:], in0=uf[:], scalar1=float(W - 1), scalar2=None, op0=ALU.is_le)
-        m9 = const.tile([P, ND], F32, name="m9")
-        nc.vector.tensor_tensor(out=m9[:], in0=ma[:], in1=mb[:], op=ALU.mult)
-        mask = const.tile([P, ND, ND], F32, name="mask")
-        nc.vector.tensor_copy(out=mask[:], in_=m9[:].unsqueeze(1).to_broadcast([P, ND, ND]))
-
+        wc = {}
+        ws = {}
+        for nm in ("k", "q"):
+            wc[nm] = const.tile([P, PASSES, C4], U32, name="wc_" + nm, align_bytes=64)
+            ws[nm] = const.tile([P, PASSES, C4], U8, name="ws_" + nm, align_bytes=64)
         qc = const.tile([P, NPIX], U32, name="qc", align_bytes=64)
         qs = const.tile([P, NPIX], U8, name="qs", align_bytes=64)
-        kc = const.tile([P, NPIX + 2 * KPAD], U32, name="kc", align_bytes=64)
-        ks = const.tile([P, NPIX + 2 * KPAD], U8, name="ks", align_bytes=64)
-        nc.vector.memset(kc[:, 0:KPAD].bitcast(I32), 0)
-        nc.vector.memset(kc[:, KPAD + NPIX :].bitcast(I32), 0)
-        nc.vector.memset(ks[:, 0:KPAD].bitcast(I32), 0)
-        nc.vector.memset(ks[:, KPAD + NPIX :].bitcast(I32), 0)
+        kc = const.tile([P, 4, KROWS * KP], U32, name="kc", align_bytes=64)
+        ks = const.tile([P, 4, KROWS * KP], U8, name="ks", align_bytes=64)
+        kc32 = kc[:].bitcast(I32)
+        ks32 = ks[:].bitcast(I32)
+        nc.vector.memset(kc32[:, :, 0 : 4 * KP], 0)
+        nc.vector.memset(kc32[:, :, (H + 4) * KP :], 0)
+        nc.vector.memset(ks32[:, :, 0:KP], 0)
+        nc.vector.memset(ks32[:, :, (H + 4) * KP // 4 :], 0)
+        kgs = []
+        for i in range(2):
+            kg = const.tile([P, 4, TR * KP * 4], BF16, name="kg%d" % i, align_bytes=64)
+            kgs.append(kg)
+            kgw = kg[:].bitcast(I32).rearrange("p b (r w) -> p b r w", w=2 * KP)
+            nc.vector.memset(kgw[:, :, :, 2 * KE :].rearrange("p b r w -> p (b r) w"), 0)
+            nc.vector.memset(kgw[:, 0, :, 0:8], 0)
+            nc.vector.memset(kgw[:, 3, :, 2 * KE - 8 : 2 * KE], 0)
         res = const.tile([P, NPIX // P, NDD], F32, name="res")
 
-        state = {"chunk": 0, "evac": 0}
+        def transposes(i):
+            w32 = raws[i][:].bitcast(F32)
+            pts = []
+            for mm in range(2):
+                pt = pst.tile([P, 512], F32, name="tp")
+                pts.append(pt)
+                for mi in range(2):
+                    for u in range(2):
+                        nc.tensor.transpose(
+                            pt[:, (2 * mi + u) * P : (2 * mi + u + 1) * P], w32[:, 2 * mm + mi, u : 256 : 2], ident[:]
+                        )
+            tps[i] = pts
 
-        def copy_on(scalar_engine, dst, src):
-            if scalar_engine:
-                nc.scalar.copy(out=dst, in_=src)
-            else:
-                nc.vector.tensor_copy(out=dst, in_=src)
-
-        def prep_w(w_ap, b_ap, nm, pieces):
-            wsb = wraw.tile([P, 4, C], BF16, name="wsb_" + nm)
-            wv = w_ap.rearrange("(p m) c -> p m c", m=4)
-            step = C // pieces
-            for i in range(pieces):
-                nc.sync.dma_start(out=wsb[:, :, i * step : (i + 1) * step], in_=wv[:, :, i * step : (i + 1) * step])
-            bb = const.tile([P, 4], BF16, name="bb_" + nm)
-            nc.sync.dma_start(out=bb[:], in_=b_ap.rearrange("(p m) -> p m", m=4))
-            bias = const.tile([P, 4], F32, name="bias_" + nm)
-            nc.vector.tensor_copy(out=bias[:], in_=bb[:])
-            wc = const.tile([P, PASSES, C4], U32, name="wc_" + nm, align_bytes=64)
-            ws = const.tile([P, PASSES, C4], U8, name="ws_" + nm, align_bytes=64)
-            w32 = wsb[:].bitcast(F32)
-            for g in range(PASSES):
-                wg = wgrp.tile([P, 4 * C4], BF16, name="wg", align_bytes=64)
-                wg32 = wg[:].bitcast(F32)
-                for mm in range(2):
-                    pt = psa.tile([P, 512], F32, name="acc")
-                    for mi in range(2):
-                        for u in range(2):
-                            nc.tensor.transpose(
-                                pt[:, (2 * mi + u) * P : (2 * mi + u + 1) * P],
-                                w32[:, 2 * mm + mi, 256 * g + u : 256 * g + 256 : 2],
-                                ident[:],
-                            )
-                    state["evac"] += 1
-                    copy_on(
-                        state["evac"] % 2 == 0,
-                        wg32[:, 512 * mm : 512 * mm + 512].rearrange("p (mi c u) -> p mi c u", mi=2, u=2),
-                        pt[:].rearrange("p (mi u c) -> p mi c u", mi=2, u=2),
-                    )
-                nc.vector.quantize_mx(out=wc[:, g, :].bitcast(FP8X4), scales=ws[:, g, :], in_=wg[:])
-            return wc, ws, bias
-
-        def regroup(scalar_engine, dst, src):
-            copy_on(
-                scalar_engine,
-                dst.rearrange("p (c i t) -> p c t i", i=4, t=4),
-                src.rearrange("p t (c i) -> p c t i", i=4),
+        def regroup_split(dst, src):
+            a = VSPLIT
+            nc.vector.tensor_copy(
+                out=dst[:, 0 : 4 * a].rearrange("p (c i t) -> p c t i", i=4, t=4),
+                in_=src[:, :, 0:a].rearrange("p t (c i) -> p c t i", i=4),
+            )
+            nc.scalar.copy(
+                out=dst[:, 4 * a :].rearrange("p (c i t) -> p c t i", i=4, t=4),
+                in_=src[:, :, a:].rearrange("p t (c i) -> p c t i", i=4),
             )
 
-        def unit(src2d, s, wpack, codes, scales):
-            wc, ws, bias = wpack
-            uc = ucp.tile([P, PASSES, UNIT], U32, name="uc", align_bytes=64)
-            us = ucp.tile([P, PASSES, UNIT], U8, name="us", align_bytes=64)
+        def stage_c(u, m):
+            nm = UNITS[u][0]
+            uc, us = ucs[u]
+            acc = psa.tile([P, UNIT], F32, name="acc")
+            accs[(u, m)] = acc
             for g in range(PASSES):
-                raw = rawp.tile([P, 4, UNIT], BF16, name="raw")
-                nc.sync.dma_start(
-                    out=raw[:],
-                    in_=src2d[512 * g : 512 * g + 512, s : s + UNIT].rearrange("(p t) w -> p t w", t=4),
-                )
-                grp = grpp.tile([P, 4 * UNIT], BF16, name="grp", align_bytes=64)
-                regroup(state["chunk"] % 8 in SCALAR_CHUNKS, grp[:], raw[:])
-                state["chunk"] += 1
-                nc.vector.quantize_mx(out=uc[:, g, :].bitcast(FP8X4), scales=us[:, g, :], in_=grp[:])
-            accs = []
-            for m in range(4):
-                acc = psa.tile([P, UNIT], F32, name="acc")
-                accs.append(acc)
-            for g in range(PASSES):
-                for m in range(4):
-                    nc.tensor.matmul_mx(
-                        out=accs[m][:],
-                        lhsT=wc[:, g, P * m : P * m + P].bitcast(FP8X4),
-                        lhsT_scale=ws[:, g, P * m : P * m + P],
-                        rhs=uc[:, g, :].bitcast(FP8X4),
-                        rhs_scale=us[:, g, :],
-                        start=(g == 0),
-                        stop=(g == PASSES - 1),
-                    )
-            pb = pbp.tile([P, 4, UNIT], BF16, name="pb")
-            for m in range(4):
-                nc.scalar.activation(out=pb[:, m, :], in_=accs[m][:], func=ACT.Identity, bias=bias[:, m : m + 1], scale=1.0)
-            g2 = pbp.tile([P, 4 * UNIT], BF16, name="g2", align_bytes=64)
-            regroup(False, g2[:], pb[:])
-            nc.vector.quantize_mx(out=codes.bitcast(FP8X4), scales=scales, in_=g2[:])
-
-        def corr_tile(t):
-            sm = pss.tile([P, 512], F32, name="sm")
-            sr = pss.tile([P, P], F32, name="sr")
-            for dst, c0, n in ((sm, 0, 512), (sr, 512, P)):
                 nc.tensor.matmul_mx(
-                    out=dst[:],
-                    lhsT=qc[:, P * t : P * t + P].bitcast(FP8X4),
-                    lhsT_scale=qs[:, P * t : P * t + P],
-                    rhs=kc[:, P * t + c0 : P * t + c0 + n].bitcast(FP8X4),
-                    rhs_scale=ks[:, P * t + c0 : P * t + c0 + n],
-                    start=True,
-                    stop=True,
+                    out=acc[:],
+                    lhsT=wc[nm][:, g, P * m : P * m + P].bitcast(FP8X4),
+                    lhsT_scale=ws[nm][:, g, P * m : P * m + P],
+                    rhs=uc[:, g, :].bitcast(FP8X4),
+                    rhs_scale=us[:, g, :],
+                    start=(g == 0),
+                    stop=(g == PASSES - 1),
                 )
-            st = stp.tile([P, SW], F32, name="st")
-            nc.scalar.copy(out=st[:, 0:512], in_=sm[:])
-            nc.vector.tensor_copy(out=st[:, 512:SW], in_=sr[:])
-            base = SLOT_BASE[t % 2]
-            nc.sync.dma_start(out=flat[base : base + P * SW].rearrange("(m c) -> m c", c=SW), in_=st[:])
-            rb = rbp.tile([P, ND * 64], F32, name="rb")
+
+        def stage_e(u, m):
+            nm = UNITS[u][0]
+            if m == 0:
+                pbs[u] = pbp.tile([P, 4, UNIT], BF16, name="pb")
+            pb = pbs[u]
+            acc = accs[(u, m)]
+            if nm == "q":
+                nc.scalar.activation(
+                    out=pb[:, m, :].rearrange("p (b r j) -> p r b j", r=TR, j=TJ),
+                    in_=acc[:].rearrange("p (r b j) -> p r b j", r=TR, j=TJ),
+                    func=ACT.Identity,
+                    bias=bias[nm][:, m : m + 1],
+                    scale=1.0,
+                )
+            else:
+                nc.scalar.activation(out=pb[:, m, :], in_=acc[:], func=ACT.Identity, bias=bias[nm][:, m : m + 1], scale=1.0)
+
+        def stage_r2(u):
+            nm, b = UNITS[u]
+            pb = pbs[u]
+            if nm == "q":
+                g2 = pbp.tile([P, 4 * UNIT], BF16, name="g2", align_bytes=64)
+                g2s[u] = g2
+                regroup_split(g2[:], pb[:])
+            else:
+                kg = kgs[b % 2]
+                for jb in range(4):
+                    e0 = 4 if jb == 0 else 0
+                    e1 = KE - 4 if jb == 3 else KE
+                    dst = kg[:, jb, :].rearrange("p (r e t) -> p r e t", e=KP, t=4)[:, :, e0:e1, :]
+                    src = pb[:].rearrange("p t (r j) -> p r j t", j=W)[:, :, TJ * jb - 4 + e0 : TJ * jb - 4 + e1, :]
+                    if jb < 2:
+                        nc.vector.tensor_copy(out=dst, in_=src)
+                    else:
+                        nc.scalar.copy(out=dst, in_=src)
+
+        def stage_q2(u):
+            nm, b = UNITS[u]
+            if nm == "q":
+                nc.vector.quantize_mx(
+                    out=qc[:, UNIT * b : UNIT * (b + 1)].bitcast(FP8X4), scales=qs[:, UNIT * b : UNIT * (b + 1)], in_=g2s[u][:]
+                )
+            else:
+                c0 = (TR * b + 4) * KP
+                for jb in range(4):
+                    nc.vector.quantize_mx(
+                        out=kc[:, jb, c0 : c0 + TR * KP].bitcast(FP8X4), scales=ks[:, jb, c0 : c0 + TR * KP], in_=kgs[b % 2][:, jb, :]
+                    )
+
+        def tile_f(ti):
+            b, jb = divmod(ti, 4)
+            sm = pss.tile([P, 512], F32, name="sm")
+            sms[ti] = sm
+            nc.tensor.matmul_mx(
+                out=sm[:],
+                lhsT=qc[:, P * ti : P * ti + P].bitcast(FP8X4),
+                lhsT_scale=qs[:, P * ti : P * ti + P],
+                rhs=kc[:, jb, TR * KP * b : TR * KP * b + 512].bitcast(FP8X4),
+                rhs_scale=ks[:, jb, TR * KP * b : TR * KP * b + 512],
+                start=True,
+                stop=True,
+            )
+
+        def tile_evac(ti):
+            st = stp.tile([P, SWID], F32, name="st")
+            sts[ti] = st
+            nc.scalar.activation(
+                out=st[:].rearrange("p (a e) -> p a e", e=KE),
+                in_=sms[ti][:].rearrange("p (a e) -> p a e", e=KP)[:, :, 0:KE],
+                func=ACT.Copy,
+                scale=1.0 / C4,
+            )
+
+        def tile_write(ti):
+            base = SLOT * (ti % NSLOT)
+            nc.sync.dma_start(out=flat[base : base + P * SWID].rearrange("(m c) -> m c", c=SWID), in_=sts[ti][:])
+
+        def tile_read(ti):
+            base = SLOT * (ti % NSLOT)
+            rb = rbp.tile([P, ND * KE], F32, name="rb")
+            rbs[ti] = rb
             nc.sync.dma_start(
                 out=rb[:, 0:RUN],
-                in_=flat[base - 4 : base - 4 + P * (SW + 1)].rearrange("(m c) -> m c", c=SW + 1)[:, 0:RUN],
+                in_=flat[base : base + SLOT]
+                .rearrange("(r z) -> r z", z=RSTEP)[:, 0 : TJ * (SWID + 1)]
+                .rearrange("r (j c) -> r j c", c=SWID + 1)[:, :, 0:RUN],
             )
-            corr = smp.tile([P, ND, ND], F32, name="corr")
-            nc.vector.tensor_tensor(
-                out=corr[:], in0=rb[:].rearrange("p (a c) -> p a c", c=64)[:, :, 0:ND], in1=mask[:], op=ALU.mult
-            )
+
+        def soft_max(ti):
             nmx = smp.tile([P, 1], F32, name="nmx")
-            nc.vector.tensor_reduce(out=nmx[:], in_=corr[:].rearrange("p a d -> p (a d)"), axis=AX.X, op=ALU.max, negate=True)
-            ex = smp.tile([P, NDD], F32, name="ex")
+            soft[ti] = [nmx]
+            nc.vector.tensor_reduce(
+                out=nmx[:], in_=rbs[ti][:].rearrange("p (a e) -> p a e", e=KE)[:, :, 0:ND], axis=AX.XY, op=ALU.max, negate=True
+            )
+
+        def soft_exp(ti):
+            ex = smp.tile([P, ND, ND], F32, name="ex")
             den = smp.tile([P, 1], F32, name="den")
             nc.scalar.activation(
-                out=ex[:], in_=corr[:].rearrange("p a d -> p (a d)"), func=ACT.Exp, bias=nmx[:, 0:1], scale=1.0, accum_out=den[:, 0:1]
+                out=ex[:],
+                in_=rbs[ti][:].rearrange("p (a e) -> p a e", e=KE)[:, :, 0:ND],
+                func=ACT.Exp,
+                bias=soft[ti][0][:, 0:1],
+                scale=1.0,
+                accum_out=den[:, 0:1],
             )
+            soft[ti].append(ex)
+            soft[ti].append(den)
+
+        def soft_recip(ti):
             rden = smp.tile([P, 1], F32, name="rden")
-            nc.vector.reciprocal(out=rden[:], in_=den[:])
-            nc.scalar.activation(out=res[:, t, :], in_=ex[:], func=ACT.Copy, scale=rden[:, 0:1])
+            nc.vector.reciprocal(out=rden[:], in_=soft[ti][2][:])
+            soft[ti].append(rden)
 
-        def k_unit(b):
-            unit(xf, UNIT * b, wk, kc[:, KPAD + UNIT * b : KPAD + UNIT * (b + 1)], ks[:, KPAD + UNIT * b : KPAD + UNIT * (b + 1)])
-
-        def q_unit(b):
-            unit(yf, UNIT * b, wq, qc[:, UNIT * b : UNIT * (b + 1)], qs[:, UNIT * b : UNIT * (b + 1)])
-            for t in range(4 * b, 4 * b + 4):
-                corr_tile(t)
-
-        wk = prep_w(key_w, key_b, "k", 4)
-        k_unit(0)
-        wq = prep_w(query_w, query_b, "q", 1)
-        k_unit(1)
-        q_unit(0)
-        k_unit(2)
-        q_unit(1)
-        k_unit(3)
-        q_unit(2)
-        q_unit(3)
-
-        for hf in range(2):
-            nc.sync.dma_start(
-                out=out2d[1024 * hf : 1024 * hf + 1024, :].rearrange("(t m) d -> m t d", m=P),
-                in_=res[:, 8 * hf : 8 * hf + 8, :],
+        def soft_scale(ti):
+            nc.scalar.activation(
+                out=res[:, ti, :], in_=soft[ti][1][:].rearrange("p a d -> p (a d)"), func=ACT.Copy, scale=soft[ti][3][:, 0:1]
             )
+
+        def tile_store(ti):
+            b, jb = divmod(ti, 4)
+            nc.sync.dma_start(
+                out=out2d[UNIT * b : UNIT * (b + 1), :].rearrange("(r j) d -> r j d", j=W)[:, TJ * jb : TJ * (jb + 1), :],
+                in_=res[:, ti, :],
+            )
+
+        def plan_unit(u, e):
+            nm, b = UNITS[u]
+            cs = max(e + 2, wready[nm] + 1)
+            for m in range(4):
+                at(cs + m, lambda u=u, m=m: stage_c(u, m))
+                at(cs + 2 + m, lambda u=u, m=m: stage_e(u, m))
+            at(cs + 6, lambda u=u: stage_r2(u))
+            at(cs + 7, lambda u=u: stage_q2(u))
+            if nm == "q":
+                z = cs + 7
+                for jb in range(4):
+                    ti = 4 * b + jb
+                    at(z + 1 + jb, lambda ti=ti: tile_f(ti))
+                    at(z + 2 + jb, lambda ti=ti: tile_evac(ti))
+                    wsl = z + 2 + jb
+                    if ti >= NSLOT:
+                        wsl = max(wsl, rslot[ti - NSLOT] + 2)
+                    rslot[ti] = wsl + 3
+                    at(wsl, lambda ti=ti: tile_write(ti))
+                    at(wsl + 3, lambda ti=ti: tile_read(ti))
+                    at(wsl + 6, lambda ti=ti: soft_max(ti))
+                    at(wsl + 7, lambda ti=ti: soft_exp(ti))
+                    at(wsl + 8, lambda ti=ti: soft_recip(ti))
+                    at(wsl + 9, lambda ti=ti: soft_scale(ti))
+
+        pend = []
+        slot = 0
+        while slot < len(items) or slot <= max(sched):
+            if slot + LOOKAHEAD < len(items):
+                emit_load(slot + LOOKAHEAD)
+            for fn in sched.get(slot, []):
+                fn()
+            if slot + 1 < len(items) and items[slot + 1][0] == "w":
+                transposes(slot + 1)
+            todo = list(pend)
+            pend = []
+            if slot < len(items):
+                kind, a, g = items[slot]
+                grp = grpp.tile([P, 4 * UNIT], BF16, name="grp", align_bytes=64)
+                if kind == "x":
+                    if g == 0:
+                        uc = ucp.tile([P, PASSES, UNIT], U32, name="uc", align_bytes=64)
+                        us = ucp.tile([P, PASSES, UNIT], U8, name="us", align_bytes=64)
+                        ucs[a] = (uc, us)
+                    regroup_split(grp[:], raws[slot][:])
+                    pend.append((grp, ucs[a][0][:, g, :], ucs[a][1][:, g, :]))
+                    if g == PASSES - 1:
+                        plan_unit(a, slot)
+                else:
+                    g32 = grp[:].bitcast(F32)
+                    nc.vector.tensor_copy(
+                        out=g32[:, 0:512].rearrange("p (mi c u) -> p mi c u", mi=2, u=2),
+                        in_=tps[slot][0][:].rearrange("p (mi u c) -> p mi c u", mi=2, u=2),
+                    )
+                    nc.scalar.copy(
+                        out=g32[:, 512:1024].rearrange("p (mi c u) -> p mi c u", mi=2, u=2),
+                        in_=tps[slot][1][:].rearrange("p (mi u c) -> p mi c u", mi=2, u=2),
+                    )
+                    pend.append((grp, wc[a][:, g, :], ws[a][:, g, :]))
+            for grp_t, codes, scales in todo:
+                nc.vector.quantize_mx(out=codes.bitcast(FP8X4), scales=scales, in_=grp_t[:])
+            slot += 1
+
+        for ti in (8, 9, 10, 11, 12, 13, 14, 0, 1, 2, 3, 4, 5, 6, 7, 15):
+            tile_store(ti)

@@ -29,16 +29,20 @@ KE = 24
 KP = 32
 KROWS = H + 8
 SWID = (TR + 8) * KE
+HROWS = TR // 2 + 8
+HWID = HROWS * KE
 RUN = KE * (ND - 1) + ND
-RSTEP = TJ * SWID + KE
+RSTEP = TJ * HWID + KE
 SLOT = TR * RSTEP
-NSLOT = 3
+NSLOT = 4
 
 FLOPS = 2 * 2 * C4 * C * NPIX + 2 * NPIX * NDD * C4
 
-VSPLIT = 328
-LOOKAHEAD = 17
-UNITS = (("k", 0), ("k", 1), ("q", 0), ("k", 2), ("q", 1), ("k", 3), ("q", 2), ("q", 3))
+VSPLIT = 304
+VSPLIT_HALF = 152
+LOOKAHEAD = 7
+UNITS = (("k", 0, 4), ("k", 4, 8), ("q", 0, 8), ("k", 12, 8), ("q", 8, 8), ("k", 20, 8), ("q", 16, 8), ("k", 28, 4), ("q", 24, 8))
+NU = len(UNITS)
 
 
 def tile_local_module_pa_kernel(tc, x, y, query_w, query_b, key_w, key_b, out):
@@ -56,7 +60,7 @@ def tile_local_module_pa_kernel(tc, x, y, query_w, query_b, key_w, key_b, out):
     for g in range(PASSES):
         items.append(("x", 1, g))
         items.append(("w", "q", g))
-    for u in range(2, len(UNITS)):
+    for u in range(2, NU):
         for g in range(PASSES):
             items.append(("x", u, g))
 
@@ -67,8 +71,8 @@ def tile_local_module_pa_kernel(tc, x, y, query_w, query_b, key_w, key_b, out):
         ucp = ctx.enter_context(tc.tile_pool(name="ucp", bufs=3))
         pbp = ctx.enter_context(tc.tile_pool(name="pbp", bufs=2))
         stp = ctx.enter_context(tc.tile_pool(name="stp", bufs=4))
-        rbp = ctx.enter_context(tc.tile_pool(name="rbp", bufs=4))
-        smp = ctx.enter_context(tc.tile_pool(name="smp", bufs=4))
+        rbp = ctx.enter_context(tc.tile_pool(name="rbp", bufs=8))
+        smp = ctx.enter_context(tc.tile_pool(name="smp", bufs=8))
         psa = ctx.enter_context(tc.psum_pool(name="psa", bufs=4))
         pst = ctx.enter_context(tc.psum_pool(name="pst", bufs=2))
         pss = ctx.enter_context(tc.psum_pool(name="pss", bufs=2))
@@ -98,16 +102,17 @@ def tile_local_module_pa_kernel(tc, x, y, query_w, query_b, key_w, key_b, out):
 
         def emit_load(i):
             kind, a, g = items[i]
-            raw = rawp.tile([P, 4, UNIT], BF16, name="raw")
-            raws[i] = raw
             if kind == "x":
-                nm, b = UNITS[a]
+                nm, r0, nr = UNITS[a]
+                raw = rawp.tile([P, 4, W * nr], BF16, name="raw")
                 nc.sync.dma_start(
                     out=raw[:],
-                    in_=src2d[nm][512 * g : 512 * g + 512, UNIT * b : UNIT * (b + 1)].rearrange("(p t) w -> p t w", t=4),
+                    in_=src2d[nm][512 * g : 512 * g + 512, W * r0 : W * (r0 + nr)].rearrange("(p t) w -> p t w", t=4),
                 )
             else:
+                raw = rawp.tile([P, 4, UNIT], BF16, name="raw")
                 nc.sync.dma_start(out=raw[:], in_=wv[a][:, :, 512 * g : 512 * g + 512])
+            raws[i] = raw
 
         ident = const.tile([P, P], F32, name="ident")
         make_identity(nc, ident[:])
@@ -159,8 +164,8 @@ def tile_local_module_pa_kernel(tc, x, y, query_w, query_b, key_w, key_b, out):
                         )
             tps[i] = pts
 
-        def regroup_split(dst, src):
-            a = VSPLIT
+        def regroup_split(dst, src, n):
+            a = VSPLIT if n == UNIT else VSPLIT_HALF
             nc.vector.tensor_copy(
                 out=dst[:, 0 : 4 * a].rearrange("p (c i t) -> p c t i", i=4, t=4),
                 in_=src[:, :, 0:a].rearrange("p t (c i) -> p c t i", i=4),
@@ -170,52 +175,68 @@ def tile_local_module_pa_kernel(tc, x, y, query_w, query_b, key_w, key_b, out):
                 in_=src[:, :, a:].rearrange("p t (c i) -> p c t i", i=4),
             )
 
-        def stage_c(u, m):
-            nm = UNITS[u][0]
+        def mx_pass(u, m, g):
+            nm, r0, nr = UNITS[u]
             uc, us = ucs[u]
-            acc = psa.tile([P, UNIT], F32, name="acc")
-            accs[(u, m)] = acc
-            for g in range(PASSES):
-                nc.tensor.matmul_mx(
-                    out=acc[:],
-                    lhsT=wc[nm][:, g, P * m : P * m + P].bitcast(FP8X4),
-                    lhsT_scale=ws[nm][:, g, P * m : P * m + P],
-                    rhs=uc[:, g, :].bitcast(FP8X4),
-                    rhs_scale=us[:, g, :],
-                    start=(g == 0),
-                    stop=(g == PASSES - 1),
-                )
+            nc.tensor.matmul_mx(
+                out=accs[(u, m)],
+                lhsT=wc[nm][:, g, P * m : P * m + P].bitcast(FP8X4),
+                lhsT_scale=ws[nm][:, g, P * m : P * m + P],
+                rhs=uc[:, g, :].bitcast(FP8X4),
+                rhs_scale=us[:, g, :],
+                start=(g == 0),
+                stop=(g == PASSES - 1),
+            )
 
-        def stage_e(u, m):
-            nm = UNITS[u][0]
+        def stage_c(u, m):
+            nr = UNITS[u][2]
+            if nr == TR:
+                acc = psa.tile([P, UNIT], F32, name="acc")
+                accs[(u, m)] = acc[:]
+            elif m % 2 == 0:
+                acc = psa.tile([P, UNIT], F32, name="acc")
+                accs[(u, m)] = acc[:, 0 : UNIT // 2]
+                accs[(u, m + 1)] = acc[:, UNIT // 2 :]
+            for g in range(PASSES):
+                mx_pass(u, m, g)
+
+        def stage_cg(u, g):
+            for m in range(4):
+                if g == 0:
+                    if m < 2:
+                        acc = pst.tile([P, UNIT], F32, name="tp")
+                    else:
+                        acc = psa.tile([P, UNIT], F32, name="acc")
+                    accs[(u, m)] = acc[:]
+                mx_pass(u, m, g)
+
+        def stage_e(u, m, on_vector):
+            nm, r0, nr = UNITS[u]
             if m == 0:
-                pbs[u] = pbp.tile([P, 4, UNIT], BF16, name="pb")
-            pb = pbs[u]
-            acc = accs[(u, m)]
+                pbs[u] = pbp.tile([P, 4, W * nr], BF16, name="pb")
+            dst = pbs[u][:, m, :]
+            src = accs[(u, m)]
             if nm == "q":
-                nc.scalar.activation(
-                    out=pb[:, m, :].rearrange("p (b r j) -> p r b j", r=TR, j=TJ),
-                    in_=acc[:].rearrange("p (r b j) -> p r b j", r=TR, j=TJ),
-                    func=ACT.Identity,
-                    bias=bias[nm][:, m : m + 1],
-                    scale=1.0,
-                )
+                dst = dst.rearrange("p (b r j) -> p r b j", r=TR, j=TJ)
+                src = src.rearrange("p (r b j) -> p r b j", r=TR, j=TJ)
+            if on_vector:
+                nc.vector.tensor_scalar(out=dst, in0=src, scalar1=bias[nm][:, m : m + 1], scalar2=None, op0=ALU.add)
             else:
-                nc.scalar.activation(out=pb[:, m, :], in_=acc[:], func=ACT.Identity, bias=bias[nm][:, m : m + 1], scale=1.0)
+                nc.scalar.activation(out=dst, in_=src, func=ACT.Identity, bias=bias[nm][:, m : m + 1], scale=1.0)
 
         def stage_r2(u):
-            nm, b = UNITS[u]
+            nm, r0, nr = UNITS[u]
             pb = pbs[u]
             if nm == "q":
                 g2 = pbp.tile([P, 4 * UNIT], BF16, name="g2", align_bytes=64)
                 g2s[u] = g2
-                regroup_split(g2[:], pb[:])
+                regroup_split(g2[:], pb[:], UNIT)
             else:
-                kg = kgs[b % 2]
+                kg = kgs[u % 2]
                 for jb in range(4):
                     e0 = 4 if jb == 0 else 0
                     e1 = KE - 4 if jb == 3 else KE
-                    dst = kg[:, jb, :].rearrange("p (r e t) -> p r e t", e=KP, t=4)[:, :, e0:e1, :]
+                    dst = kg[:, jb, 0 : nr * KP * 4].rearrange("p (r e t) -> p r e t", e=KP, t=4)[:, :, e0:e1, :]
                     src = pb[:].rearrange("p t (r j) -> p r j t", j=W)[:, :, TJ * jb - 4 + e0 : TJ * jb - 4 + e1, :]
                     if jb < 2:
                         nc.vector.tensor_copy(out=dst, in_=src)
@@ -223,16 +244,17 @@ def tile_local_module_pa_kernel(tc, x, y, query_w, query_b, key_w, key_b, out):
                         nc.scalar.copy(out=dst, in_=src)
 
         def stage_q2(u):
-            nm, b = UNITS[u]
+            nm, r0, nr = UNITS[u]
             if nm == "q":
-                nc.vector.quantize_mx(
-                    out=qc[:, UNIT * b : UNIT * (b + 1)].bitcast(FP8X4), scales=qs[:, UNIT * b : UNIT * (b + 1)], in_=g2s[u][:]
-                )
+                c0 = W * r0
+                nc.vector.quantize_mx(out=qc[:, c0 : c0 + UNIT].bitcast(FP8X4), scales=qs[:, c0 : c0 + UNIT], in_=g2s[u][:])
             else:
-                c0 = (TR * b + 4) * KP
+                c0 = (r0 + 4) * KP
                 for jb in range(4):
                     nc.vector.quantize_mx(
-                        out=kc[:, jb, c0 : c0 + TR * KP].bitcast(FP8X4), scales=ks[:, jb, c0 : c0 + TR * KP], in_=kgs[b % 2][:, jb, :]
+                        out=kc[:, jb, c0 : c0 + nr * KP].bitcast(FP8X4),
+                        scales=ks[:, jb, c0 : c0 + nr * KP],
+                        in_=kgs[u % 2][:, jb, 0 : nr * KP * 4],
                     )
 
         def tile_f(ti):
@@ -249,19 +271,23 @@ def tile_local_module_pa_kernel(tc, x, y, query_w, query_b, key_w, key_b, out):
                 stop=True,
             )
 
-        def tile_evac(ti):
+        def tile_evac(ti, on_vector):
             st = stp.tile([P, SWID], F32, name="st")
             sts[ti] = st
-            nc.scalar.activation(
-                out=st[:].rearrange("p (a e) -> p a e", e=KE),
-                in_=sms[ti][:].rearrange("p (a e) -> p a e", e=KP)[:, :, 0:KE],
-                func=ACT.Copy,
-                scale=1.0 / C4,
-            )
+            dst = st[:].rearrange("p (a e) -> p a e", e=KE)
+            src = sms[ti][:].rearrange("p (a e) -> p a e", e=KP)[:, :, 0:KE]
+            if on_vector:
+                nc.vector.tensor_scalar(out=dst, in0=src, scalar1=1.0 / C4, scalar2=None, op0=ALU.mult)
+            else:
+                nc.scalar.activation(out=dst, in_=src, func=ACT.Copy, scale=1.0 / C4)
 
         def tile_write(ti):
-            base = SLOT * (ti % NSLOT)
-            nc.sync.dma_start(out=flat[base : base + P * SWID].rearrange("(m c) -> m c", c=SWID), in_=sts[ti][:])
+            for hf in range(2):
+                base = SLOT * (ti % NSLOT) + hf * (SLOT // 2)
+                nc.sync.dma_start(
+                    out=flat[base : base + 64 * HWID].rearrange("(m c) -> m c", c=HWID),
+                    in_=sts[ti][64 * hf : 64 * hf + 64, 4 * KE * hf : 4 * KE * hf + HWID],
+                )
 
         def tile_read(ti):
             base = SLOT * (ti % NSLOT)
@@ -270,8 +296,8 @@ def tile_local_module_pa_kernel(tc, x, y, query_w, query_b, key_w, key_b, out):
             nc.sync.dma_start(
                 out=rb[:, 0:RUN],
                 in_=flat[base : base + SLOT]
-                .rearrange("(r z) -> r z", z=RSTEP)[:, 0 : TJ * (SWID + 1)]
-                .rearrange("r (j c) -> r j c", c=SWID + 1)[:, :, 0:RUN],
+                .rearrange("(r z) -> r z", z=RSTEP)[:, 0 : TJ * (HWID + 1)]
+                .rearrange("r (j c) -> r j c", c=HWID + 1)[:, :, 0:RUN],
             )
 
         def soft_max(ti):
@@ -312,30 +338,57 @@ def tile_local_module_pa_kernel(tc, x, y, query_w, query_b, key_w, key_b, out):
                 in_=res[:, ti, :],
             )
 
-        def plan_unit(u, e):
-            nm, b = UNITS[u]
-            cs = max(e + 2, wready[nm] + 1)
-            for m in range(4):
-                at(cs + m, lambda u=u, m=m: stage_c(u, m))
-                at(cs + 2 + m, lambda u=u, m=m: stage_e(u, m))
-            at(cs + 6, lambda u=u: stage_r2(u))
-            at(cs + 7, lambda u=u: stage_q2(u))
-            if nm == "q":
-                z = cs + 7
-                for jb in range(4):
-                    ti = 4 * b + jb
-                    at(z + 1 + jb, lambda ti=ti: tile_f(ti))
-                    at(z + 2 + jb, lambda ti=ti: tile_evac(ti))
-                    wsl = z + 2 + jb
+        def plan_tiles(b, z, tail):
+            for jb in range(4):
+                ti = 4 * b + jb
+                if tail:
+                    fsl = z + jb // 2
+                    esl = fsl + 1
+                    wsl = max(esl, rslot[4 * b - 1] + 1)
+                    rlag = 1
+                    slag = 1
+                else:
+                    fsl = z + 1 + jb
+                    esl = fsl + 1
+                    wsl = esl
                     if ti >= NSLOT:
                         wsl = max(wsl, rslot[ti - NSLOT] + 2)
-                    rslot[ti] = wsl + 3
-                    at(wsl, lambda ti=ti: tile_write(ti))
-                    at(wsl + 3, lambda ti=ti: tile_read(ti))
-                    at(wsl + 6, lambda ti=ti: soft_max(ti))
-                    at(wsl + 7, lambda ti=ti: soft_exp(ti))
-                    at(wsl + 8, lambda ti=ti: soft_recip(ti))
-                    at(wsl + 9, lambda ti=ti: soft_scale(ti))
+                    rlag = 3
+                    slag = 3
+                at(fsl, lambda ti=ti: tile_f(ti))
+                at(esl, lambda ti=ti: tile_evac(ti, tail and ti % 2 == 1))
+                rslot[ti] = wsl + rlag
+                at(wsl, lambda ti=ti: tile_write(ti))
+                at(wsl + rlag, lambda ti=ti: tile_read(ti))
+                at(wsl + rlag + slag, lambda ti=ti: soft_max(ti))
+                at(wsl + rlag + slag + 1, lambda ti=ti: soft_exp(ti))
+                at(wsl + rlag + slag + 2, lambda ti=ti: soft_recip(ti))
+                at(wsl + rlag + slag + 3, lambda ti=ti: soft_scale(ti))
+
+        def plan_unit(u, e):
+            nm, r0, nr = UNITS[u]
+            cs = max(e + 2, wready[nm] + 1)
+            if u == NU - 1:
+                for m in range(4):
+                    at(cs + 1, lambda u=u, m=m: stage_e(u, m, m >= 2))
+                at(cs + 2, lambda u=u: stage_r2(u))
+                at(cs + 3, lambda u=u: stage_q2(u))
+                plan_tiles(r0 // TR, cs + 3, True)
+            elif u == NU - 2:
+                for m in range(4):
+                    at(cs + m // 2, lambda u=u, m=m: stage_c(u, m))
+                    at(cs + 2 + m // 2, lambda u=u, m=m: stage_e(u, m, False))
+                at(cs + 4, lambda u=u: stage_r2(u))
+                at(cs + 5, lambda u=u: stage_q2(u))
+            else:
+                lag = 1 if u == NU - 3 else 2
+                for m in range(4):
+                    at(cs + m, lambda u=u, m=m: stage_c(u, m))
+                    at(cs + lag + m, lambda u=u, m=m: stage_e(u, m, False))
+                at(cs + lag + 4, lambda u=u: stage_r2(u))
+                at(cs + lag + 5, lambda u=u: stage_q2(u))
+                if nm == "q":
+                    plan_tiles(r0 // TR, cs + lag + 5, False)
 
         pend = []
         slot = 0
@@ -350,17 +403,21 @@ def tile_local_module_pa_kernel(tc, x, y, query_w, query_b, key_w, key_b, out):
             pend = []
             if slot < len(items):
                 kind, a, g = items[slot]
-                grp = grpp.tile([P, 4 * UNIT], BF16, name="grp", align_bytes=64)
                 if kind == "x":
+                    n = W * UNITS[a][2]
+                    grp = grpp.tile([P, 4 * n], BF16, name="grp", align_bytes=64)
                     if g == 0:
-                        uc = ucp.tile([P, PASSES, UNIT], U32, name="uc", align_bytes=64)
-                        us = ucp.tile([P, PASSES, UNIT], U8, name="us", align_bytes=64)
+                        uc = ucp.tile([P, PASSES, n], U32, name="uc", align_bytes=64)
+                        us = ucp.tile([P, PASSES, n], U8, name="us", align_bytes=64)
                         ucs[a] = (uc, us)
-                    regroup_split(grp[:], raws[slot][:])
+                    regroup_split(grp[:], raws[slot][:], n)
                     pend.append((grp, ucs[a][0][:, g, :], ucs[a][1][:, g, :]))
+                    if a == NU - 1:
+                        at(slot + 2, lambda u=a, g=g: stage_cg(u, g))
                     if g == PASSES - 1:
                         plan_unit(a, slot)
                 else:
+                    grp = grpp.tile([P, 4 * UNIT], BF16, name="grp", align_bytes=64)
                     g32 = grp[:].bitcast(F32)
                     nc.vector.tensor_copy(
                         out=g32[:, 0:512].rearrange("p (mi c u) -> p mi c u", mi=2, u=2),
@@ -375,5 +432,5 @@ def tile_local_module_pa_kernel(tc, x, y, query_w, query_b, key_w, key_b, out):
                 nc.vector.quantize_mx(out=codes.bitcast(FP8X4), scales=scales, in_=grp_t[:])
             slot += 1
 
-        for ti in (8, 9, 10, 11, 12, 13, 14, 0, 1, 2, 3, 4, 5, 6, 7, 15):
+        for ti in range(NPIX // P):
             tile_store(ti)

@@ -38,8 +38,8 @@ NSLOT = 4
 
 FLOPS = 2 * 2 * C4 * C * NPIX + 2 * NPIX * NDD * C4
 
-VSPLIT = 304
-VSPLIT_HALF = 152
+VSPLIT = 344
+VSPLIT_HALF = 176
 LOOKAHEAD = 7
 UNITS = (("k", 0, 4), ("k", 4, 8), ("q", 0, 8), ("k", 12, 8), ("q", 8, 8), ("k", 20, 8), ("q", 16, 8), ("k", 28, 4), ("q", 24, 8))
 NU = len(UNITS)

@@ -40,8 +40,10 @@ FLOPS = 2 * 2 * C4 * C * NPIX + 2 * NPIX * NDD * C4
 
 VSPLIT = 344
 VSPLIT_HALF = 176
-LOOKAHEAD = 7
-UNITS = (("k", 0, 4), ("k", 4, 8), ("q", 0, 8), ("k", 12, 8), ("q", 8, 8), ("k", 20, 8), ("q", 16, 8), ("k", 28, 4), ("q", 24, 8))
+UNITS = (("k", 0, 4), ("k", 4, 8), ("q", 0, 8), ("q", 8, 8), ("k", 12, 8), ("k", 20, 8), ("q", 16, 8), ("q", 24, 8), ("k", 28, 4))
+PAIRED = {2: (0, 16), 3: (0, 16), 4: (12, 16), 5: (12, 16), 6: (16, 16), 7: (16, 16)}
+TILES_AFTER = {2: 0, 4: 1, 6: 2, 8: 3}
+RAW_BUFS = 8
 NU = len(UNITS)
 
 
@@ -64,9 +66,35 @@ def tile_local_module_pa_kernel(tc, x, y, query_w, query_b, key_w, key_b, out):
         for g in range(PASSES):
             items.append(("x", u, g))
 
+    loads = []
+    seen = {}
+    item_load = {}
+    last_use = {}
+    for i in range(len(items)):
+        kind, a, g = items[i]
+        if kind == "x":
+            nm, r0, nr = UNITS[a]
+            lr0, lnr = PAIRED.get(a, (r0, nr))
+            key = (nm, lr0, lnr, g)
+            off = W * (r0 - lr0)
+        else:
+            key = ("w", a, 0, g)
+            off = 0
+        if key not in seen:
+            seen[key] = len(loads)
+            loads.append(key)
+        item_load[i] = (seen[key], off)
+        last_use[seen[key]] = i
+    load_at = {}
+    for n in range(RAW_BUFS, len(loads)):
+        s = last_use[n - RAW_BUFS] + 1
+        if s not in load_at:
+            load_at[s] = []
+        load_at[s].append(n)
+
     with ExitStack() as ctx:
         const = ctx.enter_context(tc.tile_pool(name="const", bufs=1))
-        rawp = ctx.enter_context(tc.tile_pool(name="rawp", bufs=LOOKAHEAD + 1))
+        rawp = ctx.enter_context(tc.tile_pool(name="rawp", bufs=RAW_BUFS))
         grpp = ctx.enter_context(tc.tile_pool(name="grpp", bufs=3))
         ucp = ctx.enter_context(tc.tile_pool(name="ucp", bufs=3))
         pbp = ctx.enter_context(tc.tile_pool(name="pbp", bufs=2))
@@ -100,19 +128,18 @@ def tile_local_module_pa_kernel(tc, x, y, query_w, query_b, key_w, key_b, out):
                 sched[slot] = []
             sched[slot].append(fn)
 
-        def emit_load(i):
-            kind, a, g = items[i]
-            if kind == "x":
-                nm, r0, nr = UNITS[a]
+        def emit_load(n):
+            nm, r0, nr, g = loads[n]
+            if nm == "w":
+                raw = rawp.tile([P, 4, UNIT], BF16, name="raw")
+                nc.sync.dma_start(out=raw[:], in_=wv[r0][:, :, 512 * g : 512 * g + 512])
+            else:
                 raw = rawp.tile([P, 4, W * nr], BF16, name="raw")
                 nc.sync.dma_start(
                     out=raw[:],
                     in_=src2d[nm][512 * g : 512 * g + 512, W * r0 : W * (r0 + nr)].rearrange("(p t) w -> p t w", t=4),
                 )
-            else:
-                raw = rawp.tile([P, 4, UNIT], BF16, name="raw")
-                nc.sync.dma_start(out=raw[:], in_=wv[a][:, :, 512 * g : 512 * g + 512])
-            raws[i] = raw
+            raws[n] = raw
 
         ident = const.tile([P, P], F32, name="ident")
         make_identity(nc, ident[:])
@@ -123,8 +150,8 @@ def tile_local_module_pa_kernel(tc, x, y, query_w, query_b, key_w, key_b, out):
             nc.scalar.dma_start(out=bbs[nm][:], in_=bv[nm])
             bias[nm] = const.tile([P, 4], F32, name="bias_" + nm)
             at(6, lambda nm=nm: nc.vector.tensor_copy(out=bias[nm][:], in_=bbs[nm][:]))
-        for i in range(LOOKAHEAD):
-            emit_load(i)
+        for n in range(RAW_BUFS):
+            emit_load(n)
 
         wc = {}
         ws = {}
@@ -152,7 +179,7 @@ def tile_local_module_pa_kernel(tc, x, y, query_w, query_b, key_w, key_b, out):
         res = const.tile([P, NPIX // P, NDD], F32, name="res")
 
         def transposes(i):
-            w32 = raws[i][:].bitcast(F32)
+            w32 = raws[item_load[i][0]][:].bitcast(F32)
             pts = []
             for mm in range(2):
                 pt = pst.tile([P, 512], F32, name="tp")
@@ -207,7 +234,7 @@ def tile_local_module_pa_kernel(tc, x, y, query_w, query_b, key_w, key_b, out):
                         acc = pst.tile([P, UNIT], F32, name="tp")
                     else:
                         acc = psa.tile([P, UNIT], F32, name="acc")
-                    accs[(u, m)] = acc[:]
+                    accs[(u, m)] = acc[:, 0 : W * UNITS[u][2]]
                 mx_pass(u, m, g)
 
         def stage_e(u, m, on_vector):
@@ -372,29 +399,23 @@ def tile_local_module_pa_kernel(tc, x, y, query_w, query_b, key_w, key_b, out):
                 for m in range(4):
                     at(cs + 1, lambda u=u, m=m: stage_e(u, m, m >= 2))
                 at(cs + 2, lambda u=u: stage_r2(u))
-                at(cs + 3, lambda u=u: stage_q2(u))
-                plan_tiles(r0 // TR, cs + 3, True)
-            elif u == NU - 2:
-                for m in range(4):
-                    at(cs + m // 2, lambda u=u, m=m: stage_c(u, m))
-                    at(cs + 2 + m // 2, lambda u=u, m=m: stage_e(u, m, False))
-                at(cs + 4, lambda u=u: stage_r2(u))
-                at(cs + 5, lambda u=u: stage_q2(u))
+                z = cs + 3
             else:
-                lag = 1 if u == NU - 3 else 2
+                lag = 1 if u >= NU - 3 else 2
                 for m in range(4):
                     at(cs + m, lambda u=u, m=m: stage_c(u, m))
                     at(cs + lag + m, lambda u=u, m=m: stage_e(u, m, False))
                 at(cs + lag + 4, lambda u=u: stage_r2(u))
-                at(cs + lag + 5, lambda u=u: stage_q2(u))
-                if nm == "q":
-                    plan_tiles(r0 // TR, cs + lag + 5, False)
+                z = cs + lag + 5
+            at(z, lambda u=u: stage_q2(u))
+            if u in TILES_AFTER:
+                plan_tiles(TILES_AFTER[u], z, u == NU - 1)
 
         pend = []
         slot = 0
         while slot < len(items) or slot <= max(sched):
-            if slot + LOOKAHEAD < len(items):
-                emit_load(slot + LOOKAHEAD)
+            for n in load_at.get(slot, []):
+                emit_load(n)
             for fn in sched.get(slot, []):
                 fn()
             if slot + 1 < len(items) and items[slot + 1][0] == "w":
@@ -410,7 +431,8 @@ def tile_local_module_pa_kernel(tc, x, y, query_w, query_b, key_w, key_b, out):
                         uc = ucp.tile([P, PASSES, n], U32, name="uc", align_bytes=64)
                         us = ucp.tile([P, PASSES, n], U8, name="us", align_bytes=64)
                         ucs[a] = (uc, us)
-                    regroup_split(grp[:], raws[slot][:], n)
+                    ld, off = item_load[slot]
+                    regroup_split(grp[:], raws[ld][:, :, off : off + n], n)
                     pend.append((grp, ucs[a][0][:, g, :], ucs[a][1][:, g, :]))
                     if a == NU - 1:
                         at(slot + 2, lambda u=a, g=g: stage_cg(u, g))

@@ -35,15 +35,17 @@ RUN = KE * (ND - 1) + ND
 RSTEP = TJ * HWID + KE
 SLOT = TR * RSTEP
 NSLOT = 4
+AJ = TR * SWID + TR * KE
+ASLOT = TJ * (AJ + 1)
+ANSLOT = 3
+LAST_B = H // TR - 1
 
 FLOPS = 2 * 2 * C4 * C * NPIX + 2 * NPIX * NDD * C4
 
 VSPLIT = 344
 VSPLIT_HALF = 176
-UNITS = (("k", 0, 4), ("k", 4, 8), ("q", 0, 8), ("q", 8, 8), ("k", 12, 8), ("k", 20, 8), ("q", 16, 8), ("q", 24, 8), ("k", 28, 4))
-PAIRED = {2: (0, 16), 3: (0, 16), 4: (12, 16), 5: (12, 16), 6: (16, 16), 7: (16, 16)}
-TILES_AFTER = {2: 0, 4: 1, 6: 2, 8: 3}
-RAW_BUFS = 8
+LOOKAHEAD = 7
+UNITS = (("k", 0, 4), ("k", 4, 8), ("q", 0, 8), ("k", 12, 8), ("q", 8, 8), ("k", 20, 8), ("q", 16, 8), ("k", 28, 4), ("q", 24, 8))
 NU = len(UNITS)
 
 
@@ -66,35 +68,9 @@ def tile_local_module_pa_kernel(tc, x, y, query_w, query_b, key_w, key_b, out):
         for g in range(PASSES):
             items.append(("x", u, g))
 
-    loads = []
-    seen = {}
-    item_load = {}
-    last_use = {}
-    for i in range(len(items)):
-        kind, a, g = items[i]
-        if kind == "x":
-            nm, r0, nr = UNITS[a]
-            lr0, lnr = PAIRED.get(a, (r0, nr))
-            key = (nm, lr0, lnr, g)
-            off = W * (r0 - lr0)
-        else:
-            key = ("w", a, 0, g)
-            off = 0
-        if key not in seen:
-            seen[key] = len(loads)
-            loads.append(key)
-        item_load[i] = (seen[key], off)
-        last_use[seen[key]] = i
-    load_at = {}
-    for n in range(RAW_BUFS, len(loads)):
-        s = last_use[n - RAW_BUFS] + 1
-        if s not in load_at:
-            load_at[s] = []
-        load_at[s].append(n)
-
     with ExitStack() as ctx:
         const = ctx.enter_context(tc.tile_pool(name="const", bufs=1))
-        rawp = ctx.enter_context(tc.tile_pool(name="rawp", bufs=RAW_BUFS))
+        rawp = ctx.enter_context(tc.tile_pool(name="rawp", bufs=LOOKAHEAD + 1))
         grpp = ctx.enter_context(tc.tile_pool(name="grpp", bufs=3))
         ucp = ctx.enter_context(tc.tile_pool(name="ucp", bufs=3))
         pbp = ctx.enter_context(tc.tile_pool(name="pbp", bufs=2))
@@ -128,18 +104,19 @@ def tile_local_module_pa_kernel(tc, x, y, query_w, query_b, key_w, key_b, out):
                 sched[slot] = []
             sched[slot].append(fn)
 
-        def emit_load(n):
-            nm, r0, nr, g = loads[n]
-            if nm == "w":
-                raw = rawp.tile([P, 4, UNIT], BF16, name="raw")
-                nc.sync.dma_start(out=raw[:], in_=wv[r0][:, :, 512 * g : 512 * g + 512])
-            else:
+        def emit_load(i):
+            kind, a, g = items[i]
+            if kind == "x":
+                nm, r0, nr = UNITS[a]
                 raw = rawp.tile([P, 4, W * nr], BF16, name="raw")
                 nc.sync.dma_start(
                     out=raw[:],
                     in_=src2d[nm][512 * g : 512 * g + 512, W * r0 : W * (r0 + nr)].rearrange("(p t) w -> p t w", t=4),
                 )
-            raws[n] = raw
+            else:
+                raw = rawp.tile([P, 4, UNIT], BF16, name="raw")
+                nc.sync.dma_start(out=raw[:], in_=wv[a][:, :, 512 * g : 512 * g + 512])
+            raws[i] = raw
 
         ident = const.tile([P, P], F32, name="ident")
         make_identity(nc, ident[:])
@@ -150,8 +127,8 @@ def tile_local_module_pa_kernel(tc, x, y, query_w, query_b, key_w, key_b, out):
             nc.scalar.dma_start(out=bbs[nm][:], in_=bv[nm])
             bias[nm] = const.tile([P, 4], F32, name="bias_" + nm)
             at(6, lambda nm=nm: nc.vector.tensor_copy(out=bias[nm][:], in_=bbs[nm][:]))
-        for n in range(RAW_BUFS):
-            emit_load(n)
+        for i in range(LOOKAHEAD):
+            emit_load(i)
 
         wc = {}
         ws = {}
@@ -179,7 +156,7 @@ def tile_local_module_pa_kernel(tc, x, y, query_w, query_b, key_w, key_b, out):
         res = const.tile([P, NPIX // P, NDD], F32, name="res")
 
         def transposes(i):
-            w32 = raws[item_load[i][0]][:].bitcast(F32)
+            w32 = raws[i][:].bitcast(F32)
             pts = []
             for mm in range(2):
                 pt = pst.tile([P, 512], F32, name="tp")
@@ -234,7 +211,7 @@ def tile_local_module_pa_kernel(tc, x, y, query_w, query_b, key_w, key_b, out):
                         acc = pst.tile([P, UNIT], F32, name="tp")
                     else:
                         acc = psa.tile([P, UNIT], F32, name="acc")
-                    accs[(u, m)] = acc[:, 0 : W * UNITS[u][2]]
+                    accs[(u, m)] = acc[:]
                 mx_pass(u, m, g)
 
         def stage_e(u, m, on_vector):
@@ -243,9 +220,12 @@ def tile_local_module_pa_kernel(tc, x, y, query_w, query_b, key_w, key_b, out):
                 pbs[u] = pbp.tile([P, 4, W * nr], BF16, name="pb")
             dst = pbs[u][:, m, :]
             src = accs[(u, m)]
-            if nm == "q":
+            if nm == "q" and r0 // TR == LAST_B:
                 dst = dst.rearrange("p (b r j) -> p r b j", r=TR, j=TJ)
                 src = src.rearrange("p (r b j) -> p r b j", r=TR, j=TJ)
+            elif nm == "q":
+                dst = dst.rearrange("p (b j r) -> p b j r", r=TR, j=TJ)
+                src = src.rearrange("p (r b j) -> p b j r", r=TR, j=TJ)
             if on_vector:
                 nc.vector.tensor_scalar(out=dst, in0=src, scalar1=bias[nm][:, m : m + 1], scalar2=None, op0=ALU.add)
             else:
@@ -309,6 +289,15 @@ def tile_local_module_pa_kernel(tc, x, y, query_w, query_b, key_w, key_b, out):
                 nc.scalar.activation(out=dst, in_=src, func=ACT.Copy, scale=1.0 / C4)
 
         def tile_write(ti):
+            if ti // 4 != LAST_B:
+                base = ASLOT * (ti % ANSLOT)
+                nc.sync.dma_start(
+                    out=flat[base : base + TJ * AJ]
+                    .rearrange("(j z) -> j z", z=AJ)[:, 0 : TR * SWID]
+                    .rearrange("j (r c) -> j r c", c=SWID),
+                    in_=sts[ti][:],
+                )
+                return
             for hf in range(2):
                 base = SLOT * (ti % NSLOT) + hf * (SLOT // 2)
                 nc.sync.dma_start(
@@ -317,9 +306,18 @@ def tile_local_module_pa_kernel(tc, x, y, query_w, query_b, key_w, key_b, out):
                 )
 
         def tile_read(ti):
-            base = SLOT * (ti % NSLOT)
             rb = rbp.tile([P, ND * KE], F32, name="rb")
             rbs[ti] = rb
+            if ti // 4 != LAST_B:
+                base = ASLOT * (ti % ANSLOT)
+                nc.sync.dma_start(
+                    out=rb[:, 0:RUN],
+                    in_=flat[base : base + ASLOT]
+                    .rearrange("(j z) -> j z", z=AJ + 1)[:, 0:AJ]
+                    .rearrange("j (r c) -> j r c", c=SWID + KE)[:, :, 0:RUN],
+                )
+                return
+            base = SLOT * (ti % NSLOT)
             nc.sync.dma_start(
                 out=rb[:, 0:RUN],
                 in_=flat[base : base + SLOT]
@@ -360,6 +358,12 @@ def tile_local_module_pa_kernel(tc, x, y, query_w, query_b, key_w, key_b, out):
 
         def tile_store(ti):
             b, jb = divmod(ti, 4)
+            if b != LAST_B:
+                nc.sync.dma_start(
+                    out=out2d[UNIT * b : UNIT * (b + 1), :].rearrange("(r j) d -> j r d", j=W)[TJ * jb : TJ * (jb + 1), :, :],
+                    in_=res[:, ti, :],
+                )
+                return
             nc.sync.dma_start(
                 out=out2d[UNIT * b : UNIT * (b + 1), :].rearrange("(r j) d -> r j d", j=W)[:, TJ * jb : TJ * (jb + 1), :],
                 in_=res[:, ti, :],
@@ -378,8 +382,8 @@ def tile_local_module_pa_kernel(tc, x, y, query_w, query_b, key_w, key_b, out):
                     fsl = z + 1 + jb
                     esl = fsl + 1
                     wsl = esl
-                    if ti >= NSLOT:
-                        wsl = max(wsl, rslot[ti - NSLOT] + 2)
+                    if ti >= ANSLOT:
+                        wsl = max(wsl, rslot[ti - ANSLOT] + 2)
                     rlag = 3
                     slag = 3
                 at(fsl, lambda ti=ti: tile_f(ti))
@@ -399,23 +403,29 @@ def tile_local_module_pa_kernel(tc, x, y, query_w, query_b, key_w, key_b, out):
                 for m in range(4):
                     at(cs + 1, lambda u=u, m=m: stage_e(u, m, m >= 2))
                 at(cs + 2, lambda u=u: stage_r2(u))
-                z = cs + 3
+                at(cs + 3, lambda u=u: stage_q2(u))
+                plan_tiles(r0 // TR, cs + 3, True)
+            elif u == NU - 2:
+                for m in range(4):
+                    at(cs + m // 2, lambda u=u, m=m: stage_c(u, m))
+                    at(cs + 2 + m // 2, lambda u=u, m=m: stage_e(u, m, False))
+                at(cs + 4, lambda u=u: stage_r2(u))
+                at(cs + 5, lambda u=u: stage_q2(u))
             else:
-                lag = 1 if u >= NU - 3 else 2
+                lag = 1 if u == NU - 3 else 2
                 for m in range(4):
                     at(cs + m, lambda u=u, m=m: stage_c(u, m))
                     at(cs + lag + m, lambda u=u, m=m: stage_e(u, m, False))
                 at(cs + lag + 4, lambda u=u: stage_r2(u))
-                z = cs + lag + 5
-            at(z, lambda u=u: stage_q2(u))
-            if u in TILES_AFTER:
-                plan_tiles(TILES_AFTER[u], z, u == NU - 1)
+                at(cs + lag + 5, lambda u=u: stage_q2(u))
+                if nm == "q":
+                    plan_tiles(r0 // TR, cs + lag + 5, False)
 
         pend = []
         slot = 0
         while slot < len(items) or slot <= max(sched):
-            for n in load_at.get(slot, []):
-                emit_load(n)
+            if slot + LOOKAHEAD < len(items):
+                emit_load(slot + LOOKAHEAD)
             for fn in sched.get(slot, []):
                 fn()
             if slot + 1 < len(items) and items[slot + 1][0] == "w":
@@ -431,8 +441,7 @@ def tile_local_module_pa_kernel(tc, x, y, query_w, query_b, key_w, key_b, out):
                         uc = ucp.tile([P, PASSES, n], U32, name="uc", align_bytes=64)
                         us = ucp.tile([P, PASSES, n], U8, name="us", align_bytes=64)
                         ucs[a] = (uc, us)
-                    ld, off = item_load[slot]
-                    regroup_split(grp[:], raws[ld][:, :, off : off + n], n)
+                    regroup_split(grp[:], raws[slot][:], n)
                     pend.append((grp, ucs[a][0][:, g, :], ucs[a][1][:, g, :]))
                     if a == NU - 1:
                         at(slot + 2, lambda u=a, g=g: stage_cg(u, g))

@@ -42,8 +42,8 @@ LAST_B = H // TR - 1
 
 FLOPS = 2 * 2 * C4 * C * NPIX + 2 * NPIX * NDD * C4
 
-VSPLIT = 344
-VSPLIT_HALF = 176
+VSPLIT = 320
+VSPLIT_HALF = 160
 LOOKAHEAD = 7
 UNITS = (("k", 0, 4), ("k", 4, 8), ("q", 0, 8), ("k", 12, 8), ("q", 8, 8), ("k", 20, 8), ("q", 16, 8), ("k", 28, 4), ("q", 24, 8))
 NU = len(UNITS)
@@ -120,6 +120,10 @@ def tile_local_module_pa_kernel(tc, x, y, query_w, query_b, key_w, key_b, out):
 
         ident = const.tile([P, P], F32, name="ident")
         make_identity(nc, ident[:])
+        warm = const.tile([P, 1], F32, name="warm")
+        nc.gpsimd.memset(warm[:], 0.0)
+        warm2 = const.tile([P, 1], F32, name="warm2")
+        nc.scalar.activation(out=warm2[:], in_=warm[:], func=ACT.Exp)
         bias = {}
         bbs = {}
         for nm in ("k", "q"):

@@ -26,7 +26,6 @@ UNIT = 512
 TR = 8
 TJ = 16
 KE = 24
-KP = 32
 KROWS = H + 8
 SWID = (TR + 8) * KE
 HROWS = TR // 2 + 8
@@ -44,6 +43,8 @@ FLOPS = 2 * 2 * C4 * C * NPIX + 2 * NPIX * NDD * C4
 
 VSPLIT = 320
 VSPLIT_HALF = 160
+VSPLIT_HEAD = 368
+VSPLIT_HEAD_HALF = 192
 LOOKAHEAD = 7
 UNITS = (("k", 0, 4), ("k", 4, 8), ("q", 0, 8), ("k", 12, 8), ("q", 8, 8), ("k", 20, 8), ("q", 16, 8), ("k", 28, 4), ("q", 24, 8))
 NU = len(UNITS)
@@ -74,7 +75,6 @@ def tile_local_module_pa_kernel(tc, x, y, query_w, query_b, key_w, key_b, out):
         grpp = ctx.enter_context(tc.tile_pool(name="grpp", bufs=3))
         ucp = ctx.enter_context(tc.tile_pool(name="ucp", bufs=3))
         pbp = ctx.enter_context(tc.tile_pool(name="pbp", bufs=2))
-        stp = ctx.enter_context(tc.tile_pool(name="stp", bufs=4))
         rbp = ctx.enter_context(tc.tile_pool(name="rbp", bufs=8))
         smp = ctx.enter_context(tc.tile_pool(name="smp", bufs=8))
         psa = ctx.enter_context(tc.psum_pool(name="psa", bufs=4))
@@ -115,7 +115,7 @@ def tile_local_module_pa_kernel(tc, x, y, query_w, query_b, key_w, key_b, out):
                 )
             else:
                 raw = rawp.tile([P, 4, UNIT], BF16, name="raw")
-                nc.sync.dma_start(out=raw[:], in_=wv[a][:, :, 512 * g : 512 * g + 512])
+                nc.sync.dma_start(out=raw[:].rearrange("p t w -> p (t w)"), in_=wv[a][:, g, :])
             raws[i] = raw
 
         ident = const.tile([P, P], F32, name="ident")
@@ -141,22 +141,20 @@ def tile_local_module_pa_kernel(tc, x, y, query_w, query_b, key_w, key_b, out):
             ws[nm] = const.tile([P, PASSES, C4], U8, name="ws_" + nm, align_bytes=64)
         qc = const.tile([P, NPIX], U32, name="qc", align_bytes=64)
         qs = const.tile([P, NPIX], U8, name="qs", align_bytes=64)
-        kc = const.tile([P, 4, KROWS * KP], U32, name="kc", align_bytes=64)
-        ks = const.tile([P, 4, KROWS * KP], U8, name="ks", align_bytes=64)
+        kc = const.tile([P, KROWS * W], U32, name="kc", align_bytes=64)
+        ks = const.tile([P, KROWS * W], U8, name="ks", align_bytes=64)
         kc32 = kc[:].bitcast(I32)
         ks32 = ks[:].bitcast(I32)
-        nc.vector.memset(kc32[:, :, 0 : 4 * KP], 0)
-        nc.vector.memset(kc32[:, :, (H + 4) * KP :], 0)
-        nc.vector.memset(ks32[:, :, 0:KP], 0)
-        nc.vector.memset(ks32[:, :, (H + 4) * KP // 4 :], 0)
-        kgs = []
-        for i in range(2):
-            kg = const.tile([P, 4, TR * KP * 4], BF16, name="kg%d" % i, align_bytes=64)
-            kgs.append(kg)
-            kgw = kg[:].bitcast(I32).rearrange("p b (r w) -> p b r w", w=2 * KP)
-            nc.vector.memset(kgw[:, :, :, 2 * KE :].rearrange("p b r w -> p (b r) w"), 0)
-            nc.vector.memset(kgw[:, 0, :, 0:8], 0)
-            nc.vector.memset(kgw[:, 3, :, 2 * KE - 8 : 2 * KE], 0)
+        nc.vector.memset(kc32[:, 0 : 4 * W], 0)
+        nc.vector.memset(kc32[:, (H + 4) * W :], 0)
+        nc.vector.memset(ks32[:, 0:W], 0)
+        nc.vector.memset(ks32[:, (H + 4) * W // 4 :], 0)
+        stf = []
+        for jb in range(4):
+            stt = const.tile([P, SWID], F32, name="st%d" % jb)
+            stf.append(stt)
+        nc.vector.memset(stf[0][:].rearrange("p (a e) -> p a e", e=KE)[:, :, 0:4], 0.0)
+        nc.vector.memset(stf[3][:].rearrange("p (a e) -> p a e", e=KE)[:, :, KE - 4 : KE], 0.0)
         res = const.tile([P, NPIX // P, NDD], F32, name="res")
 
         def transposes(i):
@@ -172,8 +170,11 @@ def tile_local_module_pa_kernel(tc, x, y, query_w, query_b, key_w, key_b, out):
                         )
             tps[i] = pts
 
-        def regroup_split(dst, src, n):
-            a = VSPLIT if n == UNIT else VSPLIT_HALF
+        def regroup_split(dst, src, n, head=False):
+            if head:
+                a = VSPLIT_HEAD if n == UNIT else VSPLIT_HEAD_HALF
+            else:
+                a = VSPLIT if n == UNIT else VSPLIT_HALF
             nc.vector.tensor_copy(
                 out=dst[:, 0 : 4 * a].rearrange("p (c i t) -> p c t i", i=4, t=4),
                 in_=src[:, :, 0:a].rearrange("p t (c i) -> p c t i", i=4),
@@ -188,8 +189,8 @@ def tile_local_module_pa_kernel(tc, x, y, query_w, query_b, key_w, key_b, out):
             uc, us = ucs[u]
             nc.tensor.matmul_mx(
                 out=accs[(u, m)],
-                lhsT=wc[nm][:, g, P * m : P * m + P].bitcast(FP8X4),
-                lhsT_scale=ws[nm][:, g, P * m : P * m + P],
+                lhsT=wc[nm][:, m, P * g : P * g + P].bitcast(FP8X4),
+                lhsT_scale=ws[nm][:, m, P * g : P * g + P],
                 rhs=uc[:, g, :].bitcast(FP8X4),
                 rhs_scale=us[:, g, :],
                 start=(g == 0),
@@ -238,21 +239,9 @@ def tile_local_module_pa_kernel(tc, x, y, query_w, query_b, key_w, key_b, out):
         def stage_r2(u):
             nm, r0, nr = UNITS[u]
             pb = pbs[u]
-            if nm == "q":
-                g2 = pbp.tile([P, 4 * UNIT], BF16, name="g2", align_bytes=64)
-                g2s[u] = g2
-                regroup_split(g2[:], pb[:], UNIT)
-            else:
-                kg = kgs[u % 2]
-                for jb in range(4):
-                    e0 = 4 if jb == 0 else 0
-                    e1 = KE - 4 if jb == 3 else KE
-                    dst = kg[:, jb, 0 : nr * KP * 4].rearrange("p (r e t) -> p r e t", e=KP, t=4)[:, :, e0:e1, :]
-                    src = pb[:].rearrange("p t (r j) -> p r j t", j=W)[:, :, TJ * jb - 4 + e0 : TJ * jb - 4 + e1, :]
-                    if jb < 2:
-                        nc.vector.tensor_copy(out=dst, in_=src)
-                    else:
-                        nc.scalar.copy(out=dst, in_=src)
+            g2 = pbp.tile([P, 4 * W * nr], BF16, name="g2", align_bytes=64)
+            g2s[u] = g2
+            regroup_split(g2[:], pb[:], W * nr)
 
         def stage_q2(u):
             nm, r0, nr = UNITS[u]
@@ -260,37 +249,43 @@ def tile_local_module_pa_kernel(tc, x, y, query_w, query_b, key_w, key_b, out):
                 c0 = W * r0
                 nc.vector.quantize_mx(out=qc[:, c0 : c0 + UNIT].bitcast(FP8X4), scales=qs[:, c0 : c0 + UNIT], in_=g2s[u][:])
             else:
-                c0 = (r0 + 4) * KP
-                for jb in range(4):
-                    nc.vector.quantize_mx(
-                        out=kc[:, jb, c0 : c0 + nr * KP].bitcast(FP8X4),
-                        scales=ks[:, jb, c0 : c0 + nr * KP],
-                        in_=kgs[u % 2][:, jb, 0 : nr * KP * 4],
-                    )
+                c0 = (r0 + 4) * W
+                nc.vector.quantize_mx(
+                    out=kc[:, c0 : c0 + nr * W].bitcast(FP8X4), scales=ks[:, c0 : c0 + nr * W], in_=g2s[u][:]
+                )
 
         def tile_f(ti):
             b, jb = divmod(ti, 4)
-            sm = pss.tile([P, 512], F32, name="sm")
-            sms[ti] = sm
-            nc.tensor.matmul_mx(
-                out=sm[:],
-                lhsT=qc[:, P * ti : P * ti + P].bitcast(FP8X4),
-                lhsT_scale=qs[:, P * ti : P * ti + P],
-                rhs=kc[:, jb, TR * KP * b : TR * KP * b + 512].bitcast(FP8X4),
-                rhs_scale=ks[:, jb, TR * KP * b : TR * KP * b + 512],
-                start=True,
-                stop=True,
-            )
+            sms[ti] = []
+            for hf in range(2):
+                if b == LAST_B and ti % 2 == 1:
+                    sm = pst.tile([P, 512], F32, name="tp")
+                else:
+                    sm = pss.tile([P, 512], F32, name="sm")
+                sms[ti].append(sm)
+                nc.tensor.matmul_mx(
+                    out=sm[:],
+                    lhsT=qc[:, P * ti : P * ti + P].bitcast(FP8X4),
+                    lhsT_scale=qs[:, P * ti : P * ti + P],
+                    rhs=kc[:, UNIT * (b + hf) : UNIT * (b + hf + 1)].bitcast(FP8X4),
+                    rhs_scale=ks[:, UNIT * (b + hf) : UNIT * (b + hf + 1)],
+                    start=True,
+                    stop=True,
+                )
 
         def tile_evac(ti, on_vector):
-            st = stp.tile([P, SWID], F32, name="st")
+            jb = ti % 4
+            st = stf[jb]
             sts[ti] = st
-            dst = st[:].rearrange("p (a e) -> p a e", e=KE)
-            src = sms[ti][:].rearrange("p (a e) -> p a e", e=KP)[:, :, 0:KE]
-            if on_vector:
-                nc.vector.tensor_scalar(out=dst, in0=src, scalar1=1.0 / C4, scalar2=None, op0=ALU.mult)
-            else:
-                nc.scalar.activation(out=dst, in_=src, func=ACT.Copy, scale=1.0 / C4)
+            e0 = 4 if jb == 0 else 0
+            e1 = KE - 4 if jb == 3 else KE
+            for hf in range(2):
+                dst = st[:].rearrange("p (a e) -> p a e", e=KE)[:, TR * hf : TR * (hf + 1), e0:e1]
+                src = sms[ti][hf][:].rearrange("p (a j) -> p a j", j=W)[:, :, TJ * jb - 4 + e0 : TJ * jb - 4 + e1]
+                if on_vector:
+                    nc.vector.tensor_scalar(out=dst, in0=src, scalar1=1.0 / C4, scalar2=None, op0=ALU.mult)
+                else:
+                    nc.scalar.activation(out=dst, in_=src, func=ACT.Copy, scale=1.0 / C4)
 
         def tile_write(ti):
             if ti // 4 != LAST_B:
@@ -445,7 +440,7 @@ def tile_local_module_pa_kernel(tc, x, y, query_w, query_b, key_w, key_b, out):
                         uc = ucp.tile([P, PASSES, n], U32, name="uc", align_bytes=64)
                         us = ucp.tile([P, PASSES, n], U8, name="us", align_bytes=64)
                         ucs[a] = (uc, us)
-                    regroup_split(grp[:], raws[slot][:], n)
+                    regroup_split(grp[:], raws[slot][:], n, a < 2)
                     pend.append((grp, ucs[a][0][:, g, :], ucs[a][1][:, g, :]))
                     if a == NU - 1:
                         at(slot + 2, lambda u=a, g=g: stage_cg(u, g))
@@ -454,7 +449,7 @@ def tile_local_module_pa_kernel(tc, x, y, query_w, query_b, key_w, key_b, out):
                 else:
                     grp = grpp.tile([P, 4 * UNIT], BF16, name="grp", align_bytes=64)
                     g32 = grp[:].bitcast(F32)
-                    nc.vector.tensor_copy(
+                    nc.scalar.copy(
                         out=g32[:, 0:512].rearrange("p (mi c u) -> p mi c u", mi=2, u=2),
                         in_=tps[slot][0][:].rearrange("p (mi u c) -> p mi c u", mi=2, u=2),
                     )

@@ -46,6 +46,8 @@ VSPLIT_HALF = 160
 VSPLIT_HEAD = 368
 VSPLIT_HEAD_HALF = 192
 LOOKAHEAD = 7
+VSPLIT_LATE = 352
+LATE_FROM = 6
 UNITS = (("k", 0, 4), ("k", 4, 8), ("q", 0, 8), ("k", 12, 8), ("q", 8, 8), ("k", 20, 8), ("q", 16, 8), ("k", 28, 4), ("q", 24, 8))
 NU = len(UNITS)
 
@@ -75,8 +77,9 @@ def tile_local_module_pa_kernel(tc, x, y, query_w, query_b, key_w, key_b, out):
         grpp = ctx.enter_context(tc.tile_pool(name="grpp", bufs=3))
         ucp = ctx.enter_context(tc.tile_pool(name="ucp", bufs=3))
         pbp = ctx.enter_context(tc.tile_pool(name="pbp", bufs=2))
-        rbp = ctx.enter_context(tc.tile_pool(name="rbp", bufs=8))
-        smp = ctx.enter_context(tc.tile_pool(name="smp", bufs=8))
+        rbp = ctx.enter_context(tc.tile_pool(name="rbp", bufs=4))
+        smp = ctx.enter_context(tc.tile_pool(name="smp", bufs=16))
+        rb4p = ctx.enter_context(tc.tile_pool(name="rb4p", bufs=3))
         psa = ctx.enter_context(tc.psum_pool(name="psa", bufs=4))
         pst = ctx.enter_context(tc.psum_pool(name="pst", bufs=2))
         pss = ctx.enter_context(tc.psum_pool(name="pss", bufs=2))
@@ -93,6 +96,8 @@ def tile_local_module_pa_kernel(tc, x, y, query_w, query_b, key_w, key_b, out):
         sts = {}
         rbs = {}
         soft = {}
+        soft4 = {}
+        rb4s = {}
         wready = {}
         for i in range(len(items)):
             if items[i][0] == "w" and items[i][2] == PASSES - 1:
@@ -170,9 +175,11 @@ def tile_local_module_pa_kernel(tc, x, y, query_w, query_b, key_w, key_b, out):
                         )
             tps[i] = pts
 
-        def regroup_split(dst, src, n, head=False):
+        def regroup_split(dst, src, n, head=False, late=False):
             if head:
                 a = VSPLIT_HEAD if n == UNIT else VSPLIT_HEAD_HALF
+            elif late:
+                a = VSPLIT_LATE * n // UNIT
             else:
                 a = VSPLIT if n == UNIT else VSPLIT_HALF
             nc.vector.tensor_copy(
@@ -241,7 +248,7 @@ def tile_local_module_pa_kernel(tc, x, y, query_w, query_b, key_w, key_b, out):
             pb = pbs[u]
             g2 = pbp.tile([P, 4 * W * nr], BF16, name="g2", align_bytes=64)
             g2s[u] = g2
-            regroup_split(g2[:], pb[:], W * nr)
+            regroup_split(g2[:], pb[:], W * nr, False, u >= LATE_FROM - 2)
 
         def stage_q2(u):
             nm, r0, nr = UNITS[u]
@@ -305,17 +312,20 @@ def tile_local_module_pa_kernel(tc, x, y, query_w, query_b, key_w, key_b, out):
                 )
 
         def tile_read(ti):
-            rb = rbp.tile([P, ND * KE], F32, name="rb")
-            rbs[ti] = rb
             if ti // 4 != LAST_B:
+                if ti % 4 == 0:
+                    rb4s[ti // 4] = rb4p.tile([P, 4, ND * KE], F32, name="rb4")
+                rbs[ti] = rb4s[ti // 4][:, ti % 4, :]
                 base = ASLOT * (ti % ANSLOT)
                 nc.sync.dma_start(
-                    out=rb[:, 0:RUN],
+                    out=rbs[ti][:, 0:RUN],
                     in_=flat[base : base + ASLOT]
                     .rearrange("(j z) -> j z", z=AJ + 1)[:, 0:AJ]
                     .rearrange("j (r c) -> j r c", c=SWID + KE)[:, :, 0:RUN],
                 )
                 return
+            rb = rbp.tile([P, ND * KE], F32, name="rb")
+            rbs[ti] = rb[:]
             base = SLOT * (ti % NSLOT)
             nc.sync.dma_start(
                 out=rb[:, 0:RUN],
@@ -326,33 +336,49 @@ def tile_local_module_pa_kernel(tc, x, y, query_w, query_b, key_w, key_b, out):
 
         def soft_max(ti):
             nmx = smp.tile([P, 1], F32, name="nmx")
-            soft[ti] = [nmx]
+            den = smp.tile([P, 1], F32, name="den")
+            rden = smp.tile([P, 1], F32, name="rden")
+            soft[ti] = [nmx[:, 0:1], None, den[:, 0:1], rden[:, 0:1]]
             nc.vector.tensor_reduce(
-                out=nmx[:], in_=rbs[ti][:].rearrange("p (a e) -> p a e", e=KE)[:, :, 0:ND], axis=AX.XY, op=ALU.max, negate=True
+                out=nmx[:], in_=rbs[ti].rearrange("p (a e) -> p a e", e=KE)[:, :, 0:ND], axis=AX.XY, op=ALU.max, negate=True
             )
+
+        def soft_max4(b):
+            nmx = rb4p.tile([P, 4], F32, name="nmx4")
+            den = rb4p.tile([P, 4], F32, name="den4")
+            rden = rb4p.tile([P, 4], F32, name="rden4")
+            soft4[b] = (den, rden)
+            for jb in range(4):
+                soft[4 * b + jb] = [nmx[:, jb : jb + 1], None, den[:, jb : jb + 1], rden[:, jb : jb + 1]]
+            nc.vector.tensor_reduce(
+                out=nmx[:],
+                in_=rb4s[b][:].rearrange("p j (a e) -> p j a e", e=KE)[:, :, :, 0:ND],
+                axis=AX.XY,
+                op=ALU.max,
+                negate=True,
+            )
+
+        def soft_recip4(b):
+            nc.vector.reciprocal(out=soft4[b][1][:], in_=soft4[b][0][:])
 
         def soft_exp(ti):
             ex = smp.tile([P, ND, ND], F32, name="ex")
-            den = smp.tile([P, 1], F32, name="den")
             nc.scalar.activation(
                 out=ex[:],
-                in_=rbs[ti][:].rearrange("p (a e) -> p a e", e=KE)[:, :, 0:ND],
+                in_=rbs[ti].rearrange("p (a e) -> p a e", e=KE)[:, :, 0:ND],
                 func=ACT.Exp,
-                bias=soft[ti][0][:, 0:1],
+                bias=soft[ti][0],
                 scale=1.0,
-                accum_out=den[:, 0:1],
+                accum_out=soft[ti][2],
             )
-            soft[ti].append(ex)
-            soft[ti].append(den)
+            soft[ti][1] = ex
 
         def soft_recip(ti):
-            rden = smp.tile([P, 1], F32, name="rden")
-            nc.vector.reciprocal(out=rden[:], in_=soft[ti][2][:])
-            soft[ti].append(rden)
+            nc.vector.reciprocal(out=soft[ti][3], in_=soft[ti][2])
 
         def soft_scale(ti):
             nc.scalar.activation(
-                out=res[:, ti, :], in_=soft[ti][1][:].rearrange("p a d -> p (a d)"), func=ACT.Copy, scale=soft[ti][3][:, 0:1]
+                out=res[:, ti, :], in_=soft[ti][1][:].rearrange("p a d -> p (a d)"), func=ACT.Copy, scale=soft[ti][3]
             )
 
         def tile_store(ti):
@@ -390,10 +416,23 @@ def tile_local_module_pa_kernel(tc, x, y, query_w, query_b, key_w, key_b, out):
                 rslot[ti] = wsl + rlag
                 at(wsl, lambda ti=ti: tile_write(ti))
                 at(wsl + rlag, lambda ti=ti: tile_read(ti))
-                at(wsl + rlag + slag, lambda ti=ti: soft_max(ti))
-                at(wsl + rlag + slag + 1, lambda ti=ti: soft_exp(ti))
-                at(wsl + rlag + slag + 2, lambda ti=ti: soft_recip(ti))
-                at(wsl + rlag + slag + 3, lambda ti=ti: soft_scale(ti))
+                t0 = wsl + rlag + slag
+                if tail:
+                    at(t0, lambda ti=ti: soft_max(ti))
+                    at(t0 + 1, lambda ti=ti: soft_exp(ti))
+                    at(t0 + 2, lambda ti=ti: soft_recip(ti))
+                    at(t0 + 3, lambda ti=ti: soft_scale(ti))
+                    if jb == 3:
+                        for bb in range(LAST_B):
+                            td = max(esl, rslot[4 * bb + 3]) + 1
+                            at(td, lambda b=bb: soft_max4(b))
+                            for k4 in range(4):
+                                at(td, lambda ti=4 * bb + k4: soft_exp(ti))
+                        for bb in range(LAST_B):
+                            td = max(esl, rslot[4 * bb + 3]) + 1
+                            at(td, lambda b=bb: soft_recip4(b))
+                            for k4 in range(4):
+                                at(td, lambda ti=4 * bb + k4: soft_scale(ti))
 
         def plan_unit(u, e):
             nm, r0, nr = UNITS[u]
@@ -440,7 +479,7 @@ def tile_local_module_pa_kernel(tc, x, y, query_w, query_b, key_w, key_b, out):
                         uc = ucp.tile([P, PASSES, n], U32, name="uc", align_bytes=64)
                         us = ucp.tile([P, PASSES, n], U8, name="us", align_bytes=64)
                         ucs[a] = (uc, us)
-                    regroup_split(grp[:], raws[slot][:], n, a < 2)
+                    regroup_split(grp[:], raws[slot][:], n, a < 2, a >= LATE_FROM)
                     pend.append((grp, ucs[a][0][:, g, :], ucs[a][1][:, g, :]))
                     if a == NU - 1:
                         at(slot + 2, lambda u=a, g=g: stage_cg(u, g))

@@ -26,7 +26,6 @@ UNIT = 512
 TR = 8
 TJ = 16
 KE = 24
-KROWS = H + 8
 SWID = (TR + 8) * KE
 HROWS = TR // 2 + 8
 HWID = HROWS * KE
@@ -50,6 +49,10 @@ VSPLIT_LATE = 352
 LATE_FROM = 6
 UNITS = (("k", 0, 4), ("k", 4, 8), ("q", 0, 8), ("k", 12, 8), ("q", 8, 8), ("k", 20, 8), ("q", 16, 8), ("k", 28, 4), ("q", 24, 8))
 NU = len(UNITS)
+
+
+def window_rows(b, hf):
+    return max(TR * hf, 4 - TR * b), min(TR * (hf + 1), H + 4 - TR * b)
 
 
 def tile_local_module_pa_kernel(tc, x, y, query_w, query_b, key_w, key_b, out):
@@ -146,20 +149,19 @@ def tile_local_module_pa_kernel(tc, x, y, query_w, query_b, key_w, key_b, out):
             ws[nm] = const.tile([P, PASSES, C4], U8, name="ws_" + nm, align_bytes=64)
         qc = const.tile([P, NPIX], U32, name="qc", align_bytes=64)
         qs = const.tile([P, NPIX], U8, name="qs", align_bytes=64)
-        kc = const.tile([P, KROWS * W], U32, name="kc", align_bytes=64)
-        ks = const.tile([P, KROWS * W], U8, name="ks", align_bytes=64)
-        kc32 = kc[:].bitcast(I32)
-        ks32 = ks[:].bitcast(I32)
-        nc.vector.memset(kc32[:, 0 : 4 * W], 0)
-        nc.vector.memset(kc32[:, (H + 4) * W :], 0)
-        nc.vector.memset(ks32[:, 0:W], 0)
-        nc.vector.memset(ks32[:, (H + 4) * W // 4 :], 0)
+        kc = const.tile([P, NPIX], U32, name="kc", align_bytes=64)
+        ks = const.tile([P, NPIX], U8, name="ks", align_bytes=64)
         stf = []
-        for jb in range(4):
-            stt = const.tile([P, SWID], F32, name="st%d" % jb)
-            stf.append(stt)
-        nc.vector.memset(stf[0][:].rearrange("p (a e) -> p a e", e=KE)[:, :, 0:4], 0.0)
-        nc.vector.memset(stf[3][:].rearrange("p (a e) -> p a e", e=KE)[:, :, KE - 4 : KE], 0.0)
+        for k3 in range(3):
+            for jb in range(4):
+                stt = const.tile([P, SWID], F32, name="st%d_%d" % (k3, jb))
+                stf.append(stt)
+                if k3 == 0:
+                    nc.vector.memset(stt[:, 0 : 4 * KE], 0.0)
+                if k3 == 2:
+                    nc.vector.memset(stt[:, SWID - 4 * KE :], 0.0)
+            nc.vector.memset(stf[4 * k3][:].rearrange("p (a e) -> p a e", e=KE)[:, :, 0:4], 0.0)
+            nc.vector.memset(stf[4 * k3 + 3][:].rearrange("p (a e) -> p a e", e=KE)[:, :, KE - 4 : KE], 0.0)
         res = const.tile([P, NPIX // P, NDD], F32, name="res")
 
         def transposes(i):
@@ -256,7 +258,7 @@ def tile_local_module_pa_kernel(tc, x, y, query_w, query_b, key_w, key_b, out):
                 c0 = W * r0
                 nc.vector.quantize_mx(out=qc[:, c0 : c0 + UNIT].bitcast(FP8X4), scales=qs[:, c0 : c0 + UNIT], in_=g2s[u][:])
             else:
-                c0 = (r0 + 4) * W
+                c0 = r0 * W
                 nc.vector.quantize_mx(
                     out=kc[:, c0 : c0 + nr * W].bitcast(FP8X4), scales=ks[:, c0 : c0 + nr * W], in_=g2s[u][:]
                 )
@@ -270,25 +272,31 @@ def tile_local_module_pa_kernel(tc, x, y, query_w, query_b, key_w, key_b, out):
                 else:
                     sm = pss.tile([P, 512], F32, name="sm")
                 sms[ti].append(sm)
+                a0, a1 = window_rows(b, hf)
+                k0 = (TR * b - 4 + a0) * W
+                k1 = (TR * b - 4 + a1) * W
                 nc.tensor.matmul_mx(
-                    out=sm[:],
+                    out=sm[:, 0 : k1 - k0],
                     lhsT=qc[:, P * ti : P * ti + P].bitcast(FP8X4),
                     lhsT_scale=qs[:, P * ti : P * ti + P],
-                    rhs=kc[:, UNIT * (b + hf) : UNIT * (b + hf + 1)].bitcast(FP8X4),
-                    rhs_scale=ks[:, UNIT * (b + hf) : UNIT * (b + hf + 1)],
+                    rhs=kc[:, k0:k1].bitcast(FP8X4),
+                    rhs_scale=ks[:, k0:k1],
                     start=True,
                     stop=True,
                 )
 
         def tile_evac(ti, on_vector):
             jb = ti % 4
-            st = stf[jb]
+            st = stf[4 * (0 if ti < 4 else (2 if ti // 4 == LAST_B else 1)) + jb]
             sts[ti] = st
             e0 = 4 if jb == 0 else 0
             e1 = KE - 4 if jb == 3 else KE
             for hf in range(2):
-                dst = st[:].rearrange("p (a e) -> p a e", e=KE)[:, TR * hf : TR * (hf + 1), e0:e1]
-                src = sms[ti][hf][:].rearrange("p (a j) -> p a j", j=W)[:, :, TJ * jb - 4 + e0 : TJ * jb - 4 + e1]
+                a0, a1 = window_rows(ti // 4, hf)
+                dst = st[:].rearrange("p (a e) -> p a e", e=KE)[:, a0:a1, e0:e1]
+                src = sms[ti][hf][:, 0 : (a1 - a0) * W].rearrange("p (a j) -> p a j", j=W)[
+                    :, :, TJ * jb - 4 + e0 : TJ * jb - 4 + e1
+                ]
                 if on_vector:
                     nc.vector.tensor_scalar(out=dst, in0=src, scalar1=1.0 / C4, scalar2=None, op0=ALU.mult)
                 else:

@@ -107,10 +107,13 @@ def tile_local_module_pa_kernel(tc, x, y, query_w, query_b, key_w, key_b, out):
                 wready[items[i][1]] = i + 1
         rslot = {}
 
-        def at(slot, fn):
+        def at(slot, fn, first=False):
             if slot not in sched:
                 sched[slot] = []
-            sched[slot].append(fn)
+            if first:
+                sched[slot].insert(0, fn)
+            else:
+                sched[slot].append(fn)
 
         def emit_load(i):
             kind, a, g = items[i]
@@ -136,11 +139,12 @@ def tile_local_module_pa_kernel(tc, x, y, query_w, query_b, key_w, key_b, out):
         bbs = {}
         for nm in ("k", "q"):
             bbs[nm] = const.tile([P, 4], BF16, name="bb_" + nm)
-            nc.scalar.dma_start(out=bbs[nm][:], in_=bv[nm])
             bias[nm] = const.tile([P, 4], F32, name="bias_" + nm)
-            at(6, lambda nm=nm: nc.vector.tensor_copy(out=bias[nm][:], in_=bbs[nm][:]))
+            at(8, lambda nm=nm: nc.vector.tensor_copy(out=bias[nm][:], in_=bbs[nm][:]))
         for i in range(LOOKAHEAD):
             emit_load(i)
+        for nm in ("k", "q"):
+            nc.sync.dma_start(out=bbs[nm][:], in_=bv[nm])
 
         wc = {}
         ws = {}
@@ -447,7 +451,7 @@ def tile_local_module_pa_kernel(tc, x, y, query_w, query_b, key_w, key_b, out):
             cs = max(e + 2, wready[nm] + 1)
             if u == NU - 1:
                 for m in range(4):
-                    at(cs + 1, lambda u=u, m=m: stage_e(u, m, m >= 2))
+                    at(cs + 1, lambda u=u, m=m: stage_e(u, m, m % 2 == 1))
                 at(cs + 2, lambda u=u: stage_r2(u))
                 at(cs + 3, lambda u=u: stage_q2(u))
                 plan_tiles(r0 // TR, cs + 3, True)

from contextlib import ExitStack

import concourse.mybir as mybir
from concourse.masks import make_identity

F32 = mybir.dt.float32
BF16 = mybir.dt.bfloat16
U32 = mybir.dt.uint32
U8 = mybir.dt.uint8
I32 = mybir.dt.int32
FP8X4 = mybir.dt.float8_e4m3fn_x4
ACT = mybir.ActivationFunctionType
ALU = mybir.AluOpType
AX = mybir.AxisListType

P = 128
C = 2048
C4 = 512
H = 32
W = 64
NPIX = H * W
ND = 9
NDD = ND * ND
PASSES = C // 512
UNIT = 512
TR = 8
TJ = 16
KE = 24
SWID = (TR + 8) * KE
HROWS = TR // 2 + 8
HWID = HROWS * KE
RUN = KE * (ND - 1) + ND
RSTEP = TJ * HWID + KE
SLOT = TR * RSTEP
NSLOT = 4
AJ = TR * SWID + TR * KE
ASLOT = TJ * (AJ + 1)
ANSLOT = 3
LAST_B = H // TR - 1

FLOPS = 2 * 2 * C4 * C * NPIX + 2 * NPIX * NDD * C4

VSPLIT = 320
VSPLIT_HALF = 160
VSPLIT_HEAD = 368
VSPLIT_HEAD_HALF = 192
LOOKAHEAD = 7
VSPLIT_LATE = 352
LATE_FROM = 6
UNITS = (("k", 0, 4), ("k", 4, 8), ("q", 0, 8), ("k", 12, 8), ("q", 8, 8), ("k", 20, 8), ("q", 16, 8), ("k", 28, 4), ("q", 24, 8))
NU = len(UNITS)


def window_rows(b, hf):
    return max(TR * hf, 4 - TR * b), min(TR * (hf + 1), H + 4 - TR * b)


def tile_local_module_pa_kernel(tc, x, y, query_w, query_b, key_w, key_b, out):
    nc = tc.nc
    src2d = {"k": x.rearrange("b c h w -> (b c) (h w)"), "q": y.rearrange("b c h w -> (b c) (h w)")}
    wv = {"k": key_w.rearrange("(p m) c -> p m c", m=4), "q": query_w.rearrange("(p m) c -> p m c", m=4)}
    bv = {"k": key_b.rearrange("(p m) -> p m", m=4), "q": query_b.rearrange("(p m) -> p m", m=4)}
    flat = out.rearrange("b h w d -> (b h w d)")
    out2d = out.rearrange("b h w d -> (b h w) d")

    items = []
    for g in range(PASSES):
        items.append(("x", 0, g))
        items.append(("w", "k", g))
    for g in range(PASSES):
        items.append(("x", 1, g))
        items.append(("w", "q", g))
    for u in range(2, NU):
        for g in range(PASSES):
            items.append(("x", u, g))

    with ExitStack() as ctx:
        const = ctx.enter_context(tc.tile_pool(name="const", bufs=1))
        rawp = ctx.enter_context(tc.tile_pool(name="rawp", bufs=LOOKAHEAD + 1))
        grpp = ctx.enter_context(tc.tile_pool(name="grpp", bufs=3))
        ucp = ctx.enter_context(tc.tile_pool(name="ucp", bufs=3))
        pbp = ctx.enter_context(tc.tile_pool(name="pbp", bufs=2))
        rbp = ctx.enter_context(tc.tile_pool(name="rbp", bufs=4))
        smp = ctx.enter_context(tc.tile_pool(name="smp", bufs=16))
        rb4p = ctx.enter_context(tc.tile_pool(name="rb4p", bufs=3))
        psa = ctx.enter_context(tc.psum_pool(name="psa", bufs=4))
        pst = ctx.enter_context(tc.psum_pool(name="pst", bufs=2))
        pss = ctx.enter_context(tc.psum_pool(name="pss", bufs=2))
        ctx.enter_context(tc.manual_schedule())

        raws = {}
        tps = {}
        sched = {}
        ucs = {}
        accs = {}
        pbs = {}
        g2s = {}
        sms = {}
        sts = {}
        rbs = {}
        soft = {}
        soft4 = {}
        rb4s = {}
        wready = {}
        for i in range(len(items)):
            if items[i][0] == "w" and items[i][2] == PASSES - 1:
                wready[items[i][1]] = i + 1
        rslot = {}

        def at(slot, fn, first=False):
            if slot not in sched:
                sched[slot] = []
            if first:
                sched[slot].insert(0, fn)
            else:
                sched[slot].append(fn)

        def emit_load(i):
            kind, a, g = items[i]
            if kind == "x":
                nm, r0, nr = UNITS[a]
                raw = rawp.tile([P, 4, W * nr], BF16, name="raw")
                nc.sync.dma_start(
                    out=raw[:],
                    in_=src2d[nm][512 * g : 512 * g + 512, W * r0 : W * (r0 + nr)].rearrange("(p t) w -> p t w", t=4),
                )
            else:
                raw = rawp.tile([P, 4, UNIT], BF16, name="raw")
                nc.sync.dma_start(out=raw[:].rearrange("p t w -> p (t w)"), in_=wv[a][:, g, :])
            raws[i] = raw

        ident = const.tile([P, P], F32, name="ident")
        make_identity(nc, ident[:])
        warm = const.tile([P, 1], F32, name="warm")
        nc.gpsimd.memset(warm[:], 0.0)
        warm2 = const.tile([P, 1], F32, name="warm2")
        nc.scalar.activation(out=warm2[:], in_=warm[:], func=ACT.Exp)
        bias = {}
        bbs = {}
        for nm in ("k", "q"):
            bbs[nm] = const.tile([P, 4], BF16, name="bb_" + nm)
            bias[nm] = const.tile([P, 4], F32, name="bias_" + nm)
            at(8, lambda nm=nm: nc.vector.tensor_copy(out=bias[nm][:], in_=bbs[nm][:]))
        for i in range(LOOKAHEAD):
            emit_load(i)
        for nm in ("k", "q"):
            nc.sync.dma_start(out=bbs[nm][:], in_=bv[nm])

        wc = {}
        ws = {}
        for nm in ("k", "q"):
            wc[nm] = const.tile([P, PASSES, C4], U32, name="wc_" + nm, align_bytes=64)
            ws[nm] = const.tile([P, PASSES, C4], U8, name="ws_" + nm, align_bytes=64)
        qc = const.tile([P, NPIX], U32, name="qc", align_bytes=64)
        qs = const.tile([P, NPIX], U8, name="qs", align_bytes=64)
        kc = const.tile([P, NPIX], U32, name="kc", align_bytes=64)
        ks = const.tile([P, NPIX], U8, name="ks", align_bytes=64)
        stf = []
        for k3 in range(3):
            for jb in range(4):
                stt = const.tile([P, SWID], F32, name="st%d_%d" % (k3, jb))
                stf.append(stt)
                if k3 == 0:
                    nc.vector.memset(stt[:, 0 : 4 * KE], 0.0)
                if k3 == 2:
                    nc.vector.memset(stt[:, SWID - 4 * KE :], 0.0)
            nc.vector.memset(stf[4 * k3][:].rearrange("p (a e) -> p a e", e=KE)[:, :, 0:4], 0.0)
            nc.vector.memset(stf[4 * k3 + 3][:].rearrange("p (a e) -> p a e", e=KE)[:, :, KE - 4 : KE], 0.0)
        res = const.tile([P, NPIX // P, NDD], F32, name="res")

        def transposes(i):
            w32 = raws[i][:].bitcast(F32)
            pts = []
            for mm in range(2):
                pt = pst.tile([P, 512], F32, name="tp")
                pts.append(pt)
                for mi in range(2):
                    for u in range(2):
                        nc.tensor.transpose(
                            pt[:, (2 * mi + u) * P : (2 * mi + u + 1) * P], w32[:, 2 * mm + mi, u : 256 : 2], ident[:]
                        )
            tps[i] = pts

        def regroup_split(dst, src, n, head=False, late=False):
            if head:
                a = VSPLIT_HEAD if n == UNIT else VSPLIT_HEAD_HALF
            elif late:
                a = VSPLIT_LATE * n // UNIT
            else:
                a = VSPLIT if n == UNIT else VSPLIT_HALF
            nc.vector.tensor_copy(
                out=dst[:, 0 : 4 * a].rearrange("p (c i t) -> p c t i", i=4, t=4),
                in_=src[:, :, 0:a].rearrange("p t (c i) -> p c t i", i=4),
            )
            nc.scalar.copy(
                out=dst[:, 4 * a :].rearrange("p (c i t) -> p c t i", i=4, t=4),
                in_=src[:, :, a:].rearrange("p t (c i) -> p c t i", i=4),
            )

        def mx_pass(u, m, g):
            nm, r0, nr = UNITS[u]
            uc, us = ucs[u]
            nc.tensor.matmul_mx(
                out=accs[(u, m)],
                lhsT=wc[nm][:, m, P * g : P * g + P].bitcast(FP8X4),
                lhsT_scale=ws[nm][:, m, P * g : P * g + P],
                rhs=uc[:, g, :].bitcast(FP8X4),
                rhs_scale=us[:, g, :],
                start=(g == 0),
                stop=(g == PASSES - 1),
            )

        def stage_c(u, m):
            nr = UNITS[u][2]
            if nr == TR:
                acc = psa.tile([P, UNIT], F32, name="acc")
                accs[(u, m)] = acc[:]
            elif m % 2 == 0:
                acc = psa.tile([P, UNIT], F32, name="acc")
                accs[(u, m)] = acc[:, 0 : UNIT // 2]
                accs[(u, m + 1)] = acc[:, UNIT // 2 :]
            for g in range(PASSES):
                mx_pass(u, m, g)

        def stage_cg(u, g):
            for m in range(4):
                if g == 0:
                    if m < 2:
                        acc = pst.tile([P, UNIT], F32, name="tp")
                    else:
                        acc = psa.tile([P, UNIT], F32, name="acc")
                    accs[(u, m)] = acc[:]
                mx_pass(u, m, g)

        def stage_e(u, m, on_vector):
            nm, r0, nr = UNITS[u]
            if m == 0:
                pbs[u] = pbp.tile([P, 4, W * nr], BF16, name="pb")
            dst = pbs[u][:, m, :]
            src = accs[(u, m)]
            if nm == "q" and r0 // TR == LAST_B:
                dst = dst.rearrange("p (b r j) -> p r b j", r=TR, j=TJ)
                src = src.rearrange("p (r b j) -> p r b j", r=TR, j=TJ)
            elif nm == "q":
                dst = dst.rearrange("p (b j r) -> p b j r", r=TR, j=TJ)
                src = src.rearrange("p (r b j) -> p b j r", r=TR, j=TJ)
            if on_vector:
                nc.vector.tensor_scalar(out=dst, in0=src, scalar1=bias[nm][:, m : m + 1], scalar2=None, op0=ALU.add)
            else:
                nc.scalar.activation(out=dst, in_=src, func=ACT.Identity, bias=bias[nm][:, m : m + 1], scale=1.0)

        def stage_r2(u):
            nm, r0, nr = UNITS[u]
            pb = pbs[u]
            g2 = pbp.tile([P, 4 * W * nr], BF16, name="g2", align_bytes=64)
            g2s[u] = g2
            regroup_split(g2[:], pb[:], W * nr, False, u >= LATE_FROM - 2)

        def stage_q2(u):
            nm, r0, nr = UNITS[u]
            if nm == "q":
                c0 = W * r0
                nc.vector.quantize_mx(out=qc[:, c0 : c0 + UNIT].bitcast(FP8X4), scales=qs[:, c0 : c0 + UNIT], in_=g2s[u][:])
            else:
                c0 = r0 * W
                nc.vector.quantize_mx(
                    out=kc[:, c0 : c0 + nr * W].bitcast(FP8X4), scales=ks[:, c0 : c0 + nr * W], in_=g2s[u][:]
                )

        def tile_f(ti):
            b, jb = divmod(ti, 4)
            sms[ti] = []
            for hf in range(2):
                if b == LAST_B and ti % 2 == 1:
                    sm = pst.tile([P, 512], F32, name="tp")
                else:
                    sm = pss.tile([P, 512], F32, name="sm")
                sms[ti].append(sm)
                a0, a1 = window_rows(b, hf)
                k0 = (TR * b - 4 + a0) * W
                k1 = (TR * b - 4 + a1) * W
                nc.tensor.matmul_mx(
                    out=sm[:, 0 : k1 - k0],
                    lhsT=qc[:, P * ti : P * ti + P].bitcast(FP8X4),
                    lhsT_scale=qs[:, P * ti : P * ti + P],
                    rhs=kc[:, k0:k1].bitcast(FP8X4),
                    rhs_scale=ks[:, k0:k1],
                    start=True,
                    stop=True,
                )

        def tile_evac(ti, on_vector):
            jb = ti % 4
            st = stf[4 * (0 if ti < 4 else (2 if ti // 4 == LAST_B else 1)) + jb]
            sts[ti] = st
            e0 = 4 if jb == 0 else 0
            e1 = KE - 4 if jb == 3 else KE
            for hf in range(2):
                a0, a1 = window_rows(ti // 4, hf)
                dst = st[:].rearrange("p (a e) -> p a e", e=KE)[:, a0:a1, e0:e1]
                src = sms[ti][hf][:, 0 : (a1 - a0) * W].rearrange("p (a j) -> p a j", j=W)[
                    :, :, TJ * jb - 4 + e0 : TJ * jb - 4 + e1
                ]
                if on_vector:
                    nc.vector.tensor_scalar(out=dst, in0=src, scalar1=1.0 / C4, scalar2=None, op0=ALU.mult)
                else:
                    nc.scalar.activation(out=dst, in_=src, func=ACT.Copy, scale=1.0 / C4)

        def tile_write(ti):
            if ti // 4 != LAST_B:
                base = ASLOT * (ti % ANSLOT)
                nc.sync.dma_start(
                    out=flat[base : base + TJ * AJ]
                    .rearrange("(j z) -> j z", z=AJ)[:, 0 : TR * SWID]
                    .rearrange("j (r c) -> j r c", c=SWID),
                    in_=sts[ti][:],
                )
                return
            for hf in range(2):
                base = SLOT * (ti % NSLOT) + hf * (SLOT // 2)
                nc.sync.dma_start(
                    out=flat[base : base + 64 * HWID].rearrange("(m c) -> m c", c=HWID),
                    in_=sts[ti][64 * hf : 64 * hf + 64, 4 * KE * hf : 4 * KE * hf + HWID],
                )

        def tile_read(ti):
            if ti // 4 != LAST_B:
                if ti % 4 == 0:
                    rb4s[ti // 4] = rb4p.tile([P, 4, ND * KE], F32, name="rb4")
                rbs[ti] = rb4s[ti // 4][:, ti % 4, :]
                base = ASLOT * (ti % ANSLOT)
                nc.sync.dma_start(
                    out=rbs[ti][:, 0:RUN],
                    in_=flat[base : base + ASLOT]
                    .rearrange("(j z) -> j z", z=AJ + 1)[:, 0:AJ]
                    .rearrange("j (r c) -> j r c", c=SWID + KE)[:, :, 0:RUN],
                )
                return
            rb = rbp.tile([P, ND * KE], F32, name="rb")
            rbs[ti] = rb[:]
            base = SLOT * (ti % NSLOT)
            nc.sync.dma_start(
                out=rb[:, 0:RUN],
                in_=flat[base : base + SLOT]
                .rearrange("(r z) -> r z", z=RSTEP)[:, 0 : TJ * (HWID + 1)]
                .rearrange("r (j c) -> r j c", c=HWID + 1)[:, :, 0:RUN],
            )

        def soft_max(ti):
            nmx = smp.tile([P, 1], F32, name="nmx")
            den = smp.tile([P, 1], F32, name="den")
            rden = smp.tile([P, 1], F32, name="rden")
            soft[ti] = [nmx[:, 0:1], None, den[:, 0:1], rden[:, 0:1]]
            nc.vector.tensor_reduce(
                out=nmx[:], in_=rbs[ti].rearrange("p (a e) -> p a e", e=KE)[:, :, 0:ND], axis=AX.XY, op=ALU.max, negate=True
            )

        def soft_max4(b):
            nmx = rb4p.tile([P, 4], F32, name="nmx4")
            den = rb4p.tile([P, 4], F32, name="den4")
            rden = rb4p.tile([P, 4], F32, name="rden4")
            soft4[b] = (den, rden)
            for jb in range(4):
                soft[4 * b + jb] = [nmx[:, jb : jb + 1], None, den[:, jb : jb + 1], rden[:, jb : jb + 1]]
            nc.vector.tensor_reduce(
                out=nmx[:],
                in_=rb4s[b][:].rearrange("p j (a e) -> p j a e", e=KE)[:, :, :, 0:ND],
                axis=AX.XY,
                op=ALU.max,
                negate=True,
            )

        def soft_recip4(b):
            nc.vector.reciprocal(out=soft4[b][1][:], in_=soft4[b][0][:])

        def soft_exp(ti):
            ex = smp.tile([P, ND, ND], F32, name="ex")
            nc.scalar.activation(
                out=ex[:],
                in_=rbs[ti].rearrange("p (a e) -> p a e", e=KE)[:, :, 0:ND],
                func=ACT.Exp,
                bias=soft[ti][0],
                scale=1.0,
                accum_out=soft[ti][2],
            )
            soft[ti][1] = ex

        def soft_recip(ti):
            nc.vector.reciprocal(out=soft[ti][3], in_=soft[ti][2])

        def soft_scale(ti):
            nc.scalar.activation(
                out=res[:, ti, :], in_=soft[ti][1][:].rearrange("p a d -> p (a d)"), func=ACT.Copy, scale=soft[ti][3]
            )

        def tile_store(ti):
            b, jb = divmod(ti, 4)
            if b != LAST_B:
                nc.sync.dma_start(
                    out=out2d[UNIT * b : UNIT * (b + 1), :].rearrange("(r j) d -> j r d", j=W)[TJ * jb : TJ * (jb + 1), :, :],
                    in_=res[:, ti, :],
                )
                return
            nc.sync.dma_start(
                out=out2d[UNIT * b : UNIT * (b + 1), :].rearrange("(r j) d -> r j d", j=W)[:, TJ * jb : TJ * (jb + 1), :],
                in_=res[:, ti, :],
            )

        def plan_tiles(b, z, tail):
            for jb in range(4):
                ti = 4 * b + jb
                if tail:
                    fsl = z + jb // 2
                    esl = fsl + 1
                    wsl = max(esl, rslot[4 * b - 1] + 1)
                    rlag = 1
                    slag = 1
                else:
                    fsl = z + 1 + jb
                    esl = fsl + 1
                    wsl = esl
                    if ti >= ANSLOT:
                        wsl = max(wsl, rslot[ti - ANSLOT] + 2)
                    rlag = 3
                    slag = 3
                at(fsl, lambda ti=ti: tile_f(ti))
                at(esl, lambda ti=ti: tile_evac(ti, tail and ti % 2 == 1))
                rslot[ti] = wsl + rlag
                at(wsl, lambda ti=ti: tile_write(ti))
                at(wsl + rlag, lambda ti=ti: tile_read(ti))
                t0 = wsl + rlag + slag
                if tail:
                    at(t0, lambda ti=ti: soft_max(ti))
                    at(t0 + 1, lambda ti=ti: soft_exp(ti))
                    at(t0 + 2, lambda ti=ti: soft_recip(ti))
                    at(t0 + 3, lambda ti=ti: soft_scale(ti))
                    if jb == 3:
                        for bb in range(LAST_B):
                            td = max(esl, rslot[4 * bb + 3]) + 1
                            at(td, lambda b=bb: soft_max4(b))
                            for k4 in range(4):
                                at(td, lambda ti=4 * bb + k4: soft_exp(ti))
                        for bb in range(LAST_B):
                            td = max(esl, rslot[4 * bb + 3]) + 1
                            at(td, lambda b=bb: soft_recip4(b))
                            for k4 in range(4):
                                at(td, lambda ti=4 * bb + k4: soft_scale(ti))

        def plan_unit(u, e):
            nm, r0, nr = UNITS[u]
            cs = max(e + 2, wready[nm] + 1)
            if u == NU - 1:
                for m in range(4):
                    at(cs + 1, lambda u=u, m=m: stage_e(u, m, m % 2 == 1))
                at(cs + 2, lambda u=u: stage_r2(u))
                at(cs + 3, lambda u=u: stage_q2(u))
                plan_tiles(r0 // TR, cs + 3, True)
            elif u == NU - 2:
                for m in range(4):
                    at(cs + m // 2, lambda u=u, m=m: stage_c(u, m))
                    at(cs + 2 + m // 2, lambda u=u, m=m: stage_e(u, m, False))
                at(cs + 4, lambda u=u: stage_r2(u))
                at(cs + 5, lambda u=u: stage_q2(u))
            else:
                lag = 1 if u == NU - 3 else 2
                for m in range(4):
                    at(cs + m, lambda u=u, m=m: stage_c(u, m))
                    at(cs + lag + m, lambda u=u, m=m: stage_e(u, m, False))
                at(cs + lag + 4, lambda u=u: stage_r2(u))
                at(cs + lag + 5, lambda u=u: stage_q2(u))
                if nm == "q":
                    plan_tiles(r0 // TR, cs + lag + 5, False)

        pend = []
        slot = 0
        while slot < len(items) or slot <= max(sched):
            if slot + LOOKAHEAD < len(items):
                emit_load(slot + LOOKAHEAD)
            for fn in sched.get(slot, []):
                fn()
            if slot + 1 < len(items) and items[slot + 1][0] == "w":
                transposes(slot + 1)
            todo = list(pend)
            pend = []
            if slot < len(items):
                kind, a, g = items[slot]
                if kind == "x":
                    n = W * UNITS[a][2]
                    grp = grpp.tile([P, 4 * n], BF16, name="grp", align_bytes=64)
                    if g == 0:
                        uc = ucp.tile([P, PASSES, n], U32, name="uc", align_bytes=64)
                        us = ucp.tile([P, PASSES, n], U8, name="us", align_bytes=64)
                        ucs[a] = (uc, us)
                    regroup_split(grp[:], raws[slot][:], n, a < 2, a >= LATE_FROM)
                    pend.append((grp, ucs[a][0][:, g, :], ucs[a][1][:, g, :]))
                    if a == NU - 1:
                        at(slot + 2, lambda u=a, g=g: stage_cg(u, g))
                    if g == PASSES - 1:
                        plan_unit(a, slot)
                else:
                    grp = grpp.tile([P, 4 * UNIT], BF16, name="grp", align_bytes=64)
                    g32 = grp[:].bitcast(F32)
                    nc.scalar.copy(
                        out=g32[:, 0:512].rearrange("p (mi c u) -> p mi c u", mi=2, u=2),
                        in_=tps[slot][0][:].rearrange("p (mi u c) -> p mi c u", mi=2, u=2),
                    )
                    nc.scalar.copy(
                        out=g32[:, 512:1024].rearrange("p (mi c u) -> p mi c u", mi=2, u=2),
                        in_=tps[slot][1][:].rearrange("p (mi u c) -> p mi c u", mi=2, u=2),
                    )
                    pend.append((grp, wc[a][:, g, :], ws[a][:, g, :]))
            for grp_t, codes, scales in todo:
                nc.vector.quantize_mx(out=codes.bitcast(FP8X4), scales=scales, in_=grp_t[:])
            slot += 1

        for ti in range(NPIX // P):
            tile_store(ti)
